import numpy as np
import ml_dtypes


def mxq(x, axis, fmt="e4m3"):
    dtype, down = {"e4m3": (ml_dtypes.float8_e4m3fn, 7), "e5m2": (ml_dtypes.float8_e5m2, 14)}[fmt]
    v = np.moveaxis(np.asarray(x, np.float32).astype(ml_dtypes.bfloat16).astype(np.float64), axis, -1)
    blocks = v.reshape(v.shape[:-1] + (-1, 32))
    amax = np.abs(blocks).max(-1, keepdims=True)
    byte = np.maximum(np.where(amax > 0, np.frexp(amax)[1] - 1 + 127, 0) - down, 1)
    scale = np.exp2(byte - 127.0)
    codes = (blocks / scale).astype(np.float32).astype(dtype).astype(np.float64)
    return np.moveaxis((codes * scale).reshape(v.shape), -1, axis)


WIDE = False


def mx_kscale(k):
    if not WIDE:
        return np.ones(k)
    levels = np.array([10, -10, 5, -5, 0])
    if k % 512:
        return np.exp2(np.random.permutation(np.resize(levels, k // 32))).repeat(32)
    a = np.empty((k // 512, 16))
    for p in range(k // 512):
        a[p, :8] = np.random.permutation(np.resize(levels, 8))
        for g in range(8):
            far = levels[np.abs(levels - a[p, g]) >= 10]
            a[p, g + 8] = far[np.random.randint(len(far))]
    return np.exp2(a.ravel()).repeat(32)


BF16 = ml_dtypes.bfloat16


def bf(x):
    return np.asarray(x, np.float32).astype(BF16)


def f64(x):
    return np.asarray(x).astype(np.float64)


B, H, L, E, QD = 16, 1, 128, 2048, 128
EPS = 1e-5


def build_decay_mask(num_heads, max_len):
    r = f64(np.arange(max_len))
    dec = np.array([1.0 - 2.0 ** (-5 - h) for h in range(num_heads)])
    expo = r[None, :] - r[:, None]
    return np.where(r[:, None] >= r[None, :], dec[:, None, None] ** expo[None], 0.0)


def draw0():
    s = mx_kscale(E)
    kv = (0.1 + 0.32 * np.random.standard_normal((B, H, L, QD))) * (0.1 + 0.32 * np.random.standard_normal((B, H, L, QD)))
    return {"x": bf(np.random.standard_normal((B, H, L, E)) * s),
            "Wq": bf(np.random.standard_normal((QD, E)) / np.sqrt(E) / s),
            "bq": bf(0.3 + 0.3 * np.random.standard_normal(QD)),
            "kv": bf(kv),
            "decay_mask": bf(build_decay_mask(H, L))}


def core(x, Wq, bq, kv, decay_mask):
    b, h, l, e = x.shape
    Q = (mxq(f64(x), 3, "e4m3") @ mxq(f64(Wq), 1, "e4m3").T) + f64(bq)
    D = f64(decay_mask)[0, :l, :l]
    y = Q * (f64(kv) @ D.T)
    mean = y.mean(axis=(2, 3), keepdims=True)
    var = ((y - mean) ** 2).mean(axis=(2, 3), keepdims=True)
    y = (y - mean) / np.sqrt(var + EPS)
    return y.reshape(b, l, -1)


def e4m3fn_bytes(y):
    return np.clip(np.asarray(y, np.float64), -448.0, 448.0).astype(np.float32).astype(ml_dtypes.float8_e4m3fn).view(np.uint8)


def e4m3fn_values(b):
    return np.asarray(b, np.uint8).view(ml_dtypes.float8_e4m3fn).astype(np.float64)


def setup_inputs():
    d = draw0()
    x0 = np.asarray(d['x']).astype(np.float64)
    s = (np.max(np.abs(x0), axis=(0, 1, 2), keepdims=True) / 448.0).astype(np.float32)
    out = {}
    for k, v in d.items():
        if k == 'x':
            out['x_bytes'] = e4m3fn_bytes(x0 / s.astype(np.float64))
            out['x_scale'] = s
        else:
            out[k] = v
    return out


def reference(x_bytes, x_scale, Wq, bq, kv, decay_mask):
    return core(e4m3fn_values(x_bytes) * x_scale.astype(np.float64), Wq, bq, kv, decay_mask)

@@ -1,0 +1,355 @@
+from contextlib import ExitStack
+
+import concourse.mybir as mybir
+from concourse.masks import make_identity
+
+F32 = mybir.dt.float32
+BF16 = mybir.dt.bfloat16
+U32 = mybir.dt.uint32
+U8 = mybir.dt.uint8
+FP8 = mybir.dt.float8_e4m3fn
+FP8X4 = mybir.dt.float8_e4m3fn_x4
+ALU = mybir.AluOpType
+ACT = mybir.ActivationFunctionType
+
+NS, L, E, QD = 16, 128, 2048, 128
+P = 128
+K_PASS = 512
+PASSES = E // K_PASS
+EPS = 1e-5
+COUNT = L * QD
+
+FLOPS = 2 * NS * L * E * QD + 2 * NS * L * QD * L
+
+GROUPS = [[0, 1, 2, 3], [4, 5, 6, 7], [8, 9, 10, 11], [12, 13], [14, 15]]
+LAST = len(GROUPS) - 1
+KV_TICK = [1, 3, 7, 11]
+
+
+def pieces(n):
+    if n == 0:
+        return [(g, g + 1) for g in range(PASSES)]
+    return [(0, 2), (2, 4)]
+
+
+def tile_parallelretention_pb_kernel(tc, x_bytes, x_scale, Wq, bq, kv, decay_mask, out):
+    nc = tc.nc
+    with ExitStack() as ctx:
+        const = ctx.enter_context(tc.tile_pool(name="const", bufs=1))
+        held = ctx.enter_context(tc.tile_pool(name="held", bufs=1))
+        work = ctx.enter_context(tc.tile_pool(name="work", bufs=3))
+        small = ctx.enter_context(tc.tile_pool(name="small", bufs=2))
+        psum = ctx.enter_context(tc.psum_pool(name="psum", bufs=1))
+        ctx.enter_context(tc.manual_schedule())
+
+        sct = const.tile([P, PASSES, 4], F32, name="sct")
+        nc.scalar.dma_start(out=sct[:], in_=x_scale.rearrange("a b c (g p t) -> p (a b c g) t", p=P, t=4))
+        xb = []
+        for n in range(NS):
+            xb_n = held.tile([P, E], U8, name="xb%d" % n)
+            xb.append(xb_n)
+        for c in range(PASSES):
+            cols = slice(K_PASS * c, K_PASS * (c + 1))
+            nc.sync.dma_start(out=xb[0][:, cols], in_=x_bytes[0, 0, :, cols])
+        w_sb = const.tile([P, E], BF16, name="w_sb")
+        nc.sync.dma_start(out=xb[1][:], in_=x_bytes[1, 0, :, :])
+        nc.sync.dma_start(out=w_sb[:], in_=Wq[:, :])
+        nc.sync.dma_start(out=xb[2][:], in_=x_bytes[2, 0, :, :])
+        d_sb = const.tile([P, L], BF16, name="d_sb")
+        nc.sync.dma_start(out=d_sb[:], in_=decay_mask.rearrange("o q k -> (o q) k"))
+        kv_sb = const.tile([P, NS, L], BF16, name="kv_sb")
+        nc.sync.dma_start(out=kv_sb[:], in_=kv.rearrange("n o l k -> l (n o) k"))
+        bq_col = const.tile([P, 1], BF16, name="bq_col")
+        nc.sync.dma_start(out=bq_col[:], in_=bq.rearrange("(p o) -> p o", o=1))
+        for n in range(3, NS):
+            nc.sync.dma_start(out=xb[n][:], in_=x_bytes[n, 0, :, :])
+
+        one = const.tile([P, 1], F32, name="one")
+        nc.gpsimd.memset(one[:], 1.0)
+        warm = const.tile([P, 1], F32, name="warm")
+        nc.scalar.activation(out=warm[:], in_=one[:], func=ACT.Sqrt)
+        ident32 = const.tile([P, P], F32, name="ident32")
+        make_identity(nc, ident32[:])
+        ident16 = const.tile([P, P], BF16, name="ident16")
+        make_identity(nc, ident16[:])
+        neg_avg = const.tile([P, P], F32, name="neg_avg")
+        nc.gpsimd.memset(neg_avg[:], -1.0 / COUNT)
+        pos_avg = const.tile([P, P], F32, name="pos_avg")
+        nc.gpsimd.memset(pos_avg[:], 1.0 / COUNT)
+        eps = const.tile([P, 1], F32, name="eps")
+        nc.gpsimd.memset(eps[:], EPS)
+
+        w_grouped = const.tile([P, E], BF16, name="w_grouped", align_bytes=64)
+        w_codes = const.tile([P, E // 4], U32, name="w_codes", align_bytes=64)
+        w_scales = const.tile([P, E // 4], U8, name="w_scales", align_bytes=64)
+        d_t = const.tile([P, P], BF16, name="d_t")
+        g_sb = const.tile([P, NS * L], F32, name="g_sb")
+
+        xs = {}
+        banks = {}
+        grouped = {}
+        codes = {}
+        scales = {}
+        q_bank = {}
+        ep = {}
+        kv_state = {}
+        group_of = {}
+        for gi, group in enumerate(GROUPS):
+            ep[gi] = {}
+            for n in group:
+                group_of[n] = gi
+
+        def widen(n):
+            xs_n = work.tile([P, E], BF16, name="xs")
+            xs[n] = xs_n
+            for g0, g1 in pieces(n):
+                cols = slice(K_PASS * g0, K_PASS * g1)
+                nc.scalar.copy(out=xs_n[:, cols], in_=xb[n][:, cols].bitcast(FP8))
+
+        def turn(words, parts):
+            tiles = []
+            for g0, g1 in parts:
+                np_ = g1 - g0
+                xt = psum.tile([P, 512], F32, tag="xt", bufs=3, name="xt")
+                for gi in range(np_):
+                    for u in range(2):
+                        s = np_ * u + gi
+                        lo = 256 * (g0 + gi)
+                        nc.tensor.transpose(
+                            out=xt[:, 128 * s : 128 * (s + 1)],
+                            in_=words[:, lo + u : lo + 256 : 2],
+                            identity=ident32[:],
+                        )
+                tiles.append(xt)
+            return tiles
+
+        def scale_out(n, i):
+            if i == 0:
+                grouped_n = work.tile([P, E], BF16, name="grouped", align_bytes=64)
+                grouped[n] = grouped_n
+            g0, g1 = pieces(n)[i]
+            np_ = g1 - g0
+            nc.vector.tensor_tensor(
+                out=grouped[n][:, 512 * g0 : 512 * g1].rearrange("p (g r u e) -> p g r u e", g=np_, u=2, e=2),
+                in0=banks[n][i][:, 0 : 256 * np_].bitcast(BF16).rearrange(
+                    "p (u g r e) -> p g r u e", u=2, g=np_, e=2
+                ),
+                in1=sct[:, g0:g1, :].rearrange("p g (o u e) -> p g o u e", o=1, u=2).to_broadcast(
+                    [P, np_, 128, 2, 2]
+                ),
+                op=ALU.mult,
+            )
+
+        def quantize_x(n, g0, g1):
+            if g0 == 0:
+                codes_n = work.tile([P, E // 4], U32, name="codes", align_bytes=64)
+                scales_n = work.tile([P, E // 4], U8, name="scales", align_bytes=64)
+                codes[n] = codes_n
+                scales[n] = scales_n
+            nc.vector.quantize_mx(
+                out=codes[n][:, 128 * g0 : 128 * g1].bitcast(FP8X4),
+                scales=scales[n][:, 128 * g0 : 128 * g1],
+                in_=grouped[n][:, 512 * g0 : 512 * g1],
+            )
+
+        def multiply(n):
+            gi = group_of[n]
+            j = n - GROUPS[gi][0]
+            if j == 0:
+                qp = psum.tile([P, 512], F32, tag="q", bufs=2, name="qp")
+                q_bank[gi] = qp
+            for g in range(PASSES):
+                gc = slice(128 * g, 128 * (g + 1))
+                nc.tensor.matmul_mx(
+                    out=q_bank[gi][:, 128 * j : 128 * (j + 1)],
+                    lhsT=w_codes[:, gc].bitcast(FP8X4),
+                    lhsT_scale=w_scales[:, gc],
+                    rhs=codes[n][:, gc].bitcast(FP8X4),
+                    rhs_scale=scales[n][:, gc],
+                    start=(g == 0),
+                    stop=(g == PASSES - 1),
+                )
+
+        def product(gi):
+            m = len(GROUPS[gi])
+            n0 = GROUPS[gi][0]
+            w = 128 * m
+            y = work.tile([P, 512], F32, name="y")
+            ep[gi]["y"] = y
+            if gi < LAST:
+                nc.vector.scalar_tensor_tensor(
+                    out=y[:, 0:w],
+                    in0=q_bank[gi][:, 0:w],
+                    scalar=bq_col[:, 0:1],
+                    in1=g_sb[:, 128 * n0 : 128 * n0 + w],
+                    op0=ALU.add,
+                    op1=ALU.mult,
+                )
+            else:
+                s1 = small.tile([P, 4], F32, name="s1")
+                ep[gi]["s1"] = s1
+                for j in range(m):
+                    nc.vector.scalar_tensor_tensor(
+                        out=y[:, 128 * j : 128 * (j + 1)],
+                        in0=q_bank[gi][:, 128 * j : 128 * (j + 1)],
+                        scalar=bq_col[:, 0:1],
+                        in1=g_sb[:, 128 * (n0 + j) : 128 * (n0 + j + 1)],
+                        op0=ALU.add,
+                        op1=ALU.mult,
+                        accum_out=s1[:, j : j + 1],
+                    )
+
+        def turn_back(gi):
+            y = ep[gi]["y"]
+            yt = psum.tile([P, 512], F32, tag="yt", bufs=2, name="yt")
+            ep[gi]["yt"] = yt
+            for j in range(len(GROUPS[gi])):
+                nc.tensor.transpose(
+                    out=yt[:, 128 * j : 128 * (j + 1)], in_=y[:, 128 * j : 128 * (j + 1)], identity=ident32[:]
+                )
+
+        def sums(gi):
+            y = ep[gi]["y"]
+            s1 = small.tile([P, 4], F32, name="s1")
+            ep[gi]["s1"] = s1
+            for j in range(len(GROUPS[gi])):
+                junk = work.tile([P, 128], F32, name="junk")
+                nc.scalar.activation(
+                    out=junk[:], in_=y[:, 128 * j : 128 * (j + 1)], func=ACT.Identity, accum_out=s1[:, j : j + 1]
+                )
+
+        def mean_and_squares(gi):
+            m = len(GROUPS[gi])
+            y = ep[gi]["y"]
+            st = psum.tile([P, 8], F32, tag="st", bufs=1, name="st")
+            ep[gi]["st"] = st
+            nc.tensor.matmul(out=st[:, 0:m], lhsT=neg_avg[:], rhs=ep[gi]["s1"][:, 0:m], start=True, stop=True)
+            nm = small.tile([P, 4], F32, name="nm")
+            ep[gi]["nm"] = nm
+            nc.scalar.copy(out=nm[:, 0:m], in_=st[:, 0:m])
+            s2 = small.tile([P, 4], F32, name="s2")
+            ep[gi]["s2"] = s2
+            for j in range(m):
+                junk = work.tile([P, 128], F32, name="junk")
+                nc.scalar.activation(
+                    out=junk[:],
+                    in_=y[:, 128 * j : 128 * (j + 1)],
+                    func=ACT.Square,
+                    bias=nm[:, j : j + 1],
+                    accum_out=s2[:, j : j + 1],
+                )
+
+        def deviation(gi):
+            m = len(GROUPS[gi])
+            st = ep[gi]["st"]
+            nc.tensor.matmul(out=st[:, 4 : 4 + m], lhsT=pos_avg[:], rhs=ep[gi]["s2"][:, 0:m], start=True, stop=True)
+            sd = small.tile([P, 4], F32, name="sd")
+            ep[gi]["sd"] = sd
+            nc.scalar.activation(out=sd[:, 0:m], in_=st[:, 4 : 4 + m], func=ACT.Sqrt, bias=eps[:, 0:1])
+
+        def factors(gi):
+            m = len(GROUPS[gi])
+            rs = small.tile([P, 4], F32, name="rs")
+            nr = small.tile([P, 4], F32, name="nr")
+            ep[gi]["rs"] = rs
+            ep[gi]["nr"] = nr
+            nc.vector.reciprocal(out=rs[:, 0:m], in_=ep[gi]["sd"][:, 0:m])
+            if gi < LAST:
+                nc.vector.tensor_tensor(out=nr[:, 0:m], in0=ep[gi]["nm"][:, 0:m], in1=rs[:, 0:m], op=ALU.mult)
+
+        def finish(gi):
+            m = len(GROUPS[gi])
+            n0 = GROUPS[gi][0]
+            o = work.tile([P, 4, 128], F32, name="o")
+            for j in range(m):
+                if gi < LAST:
+                    nc.scalar.activation(
+                        out=o[:, j, :],
+                        in_=ep[gi]["yt"][:, 128 * j : 128 * (j + 1)],
+                        func=ACT.Identity,
+                        scale=ep[gi]["rs"][:, j : j + 1],
+                        bias=ep[gi]["nr"][:, j : j + 1],
+                    )
+                else:
+                    nc.vector.tensor_scalar(
+                        out=o[:, j, :],
+                        in0=ep[gi]["yt"][:, 128 * j : 128 * (j + 1)],
+                        scalar1=ep[gi]["nm"][:, j : j + 1],
+                        scalar2=ep[gi]["rs"][:, j : j + 1],
+                        op0=ALU.add,
+                        op1=ALU.mult,
+                    )
+            nc.sync.dma_start(out=out[n0 : n0 + m].rearrange("n l q -> l n q"), in_=o[:, 0:m, :])
+
+        def stage(gi, k):
+            return k - (GROUPS[gi][-1] + 2)
+
+        n_groups = len(GROUPS)
+        for k in range(-2, NS + 4):
+            for gi in range(n_groups):
+                if stage(gi, k) == 1:
+                    mean_and_squares(gi)
+            for c in range(4):
+                if k == KV_TICK[c] + 1:
+                    kv_t = work.tile([P, 512], BF16, name="kv_t")
+                    kv_state[c] = kv_t
+                    nc.scalar.copy(out=kv_t[:], in_=kv_state["ps"][:])
+            if k == 0:
+                for i, (g0, g1) in enumerate(pieces(1)):
+                    nc.scalar.copy(
+                        out=w_grouped[:, 512 * g0 : 512 * g1].bitcast(F32).rearrange(
+                            "p (g r u) -> p g r u", g=2, u=2
+                        ),
+                        in_=banks["w"][i][:].rearrange("p (u g r) -> p g r u", u=2, g=2),
+                    )
+            if 0 <= k + 2 < NS:
+                widen(k + 2)
+            if 0 <= k + 1 < NS:
+                banks[k + 1] = turn(xs[k + 1][:].bitcast(F32), pieces(k + 1))
+            if k == -1:
+                banks["w"] = turn(w_sb[:].bitcast(F32), pieces(1))
+            if 0 <= k < NS:
+                scale_out(k, 0)
+            if 0 <= k - 1 < NS - 1:
+                quantize_x(k - 1, 0, PASSES)
+            if k - 1 == NS - 1:
+                quantize_x(k - 1, 0, 2)
+                quantize_x(k - 1, 2, PASSES)
+            if k == 1:
+                nc.vector.quantize_mx(out=w_codes[:].bitcast(FP8X4), scales=w_scales[:], in_=w_grouped[:])
+            for gi in range(n_groups):
+                if stage(gi, k) == 0:
+                    product(gi)
+            for gi in range(n_groups):
+                if stage(gi, k) == 2:
+                    factors(gi)
+            if 0 <= k < NS:
+                for i in range(1, len(pieces(k))):
+                    scale_out(k, i)
+            if 0 <= k - 1 < NS:
+                multiply(k - 1)
+            for gi in range(n_groups):
+                if stage(gi, k) == 0:
+                    turn_back(gi)
+                    if gi < LAST:
+                        sums(gi)
+                if stage(gi, k) == 1:
+                    deviation(gi)
+                if stage(gi, k) == 2:
+                    finish(gi)
+            for c in range(4):
+                if k == KV_TICK[c] + 1:
+                    gp = psum.tile([P, 512], F32, tag="yt", bufs=2, name="gp")
+                    nc.tensor.matmul(out=gp[:], lhsT=d_t[:], rhs=kv_state[c][:], start=True, stop=True)
+                    nc.scalar.copy(out=g_sb[:, 512 * c : 512 * (c + 1)], in_=gp[:])
+                if k == KV_TICK[c]:
+                    kt = psum.tile([P, 512], BF16, tag="yt", bufs=2, name="kt")
+                    kv_state["ps"] = kt
+                    for j in range(4):
+                        nc.tensor.transpose(
+                            out=kt[:, 128 * j : 128 * (j + 1)], in_=kv_sb[:, 4 * c + j, :], identity=ident16[:]
+                        )
+            if k == 0:
+                dt_ps = psum.tile([P, 512], BF16, tag="yt", bufs=2, name="dt_ps")
+                nc.tensor.transpose(out=dt_ps[:, 0:P], in_=d_sb[:], identity=ident16[:])
+                nc.scalar.copy(out=d_t[:], in_=dt_ps[:, 0:P])

@@ -16,14 +16,15 @@ NS, L, E, QD = 16, 128, 2048, 128
 P = 128
 K_PASS = 512
 PASSES = E // K_PASS
+HALF = E // 2
 EPS = 1e-5
 COUNT = L * QD
 
 FLOPS = 2 * NS * L * E * QD + 2 * NS * L * QD * L
 
-GROUPS = [[0, 1, 2, 3], [4, 5, 6, 7], [8, 9, 10, 11], [12, 13], [14, 15]]
+GROUPS = [[0, 1, 2, 3], [4, 5, 6, 7], [8, 9, 10, 11], [12, 13, 14], [15]]
+VECTOR_SUMS = (3, 4)
 LAST = len(GROUPS) - 1
-KV_TICK = [1, 3, 7, 11]
 
 
 def pieces(n):
@@ -48,21 +49,39 @@ def tile_parallelretention_pb_kernel(tc, x_bytes, x_scale, Wq, bq, kv, decay_mas
         for n in range(NS):
             xb_n = held.tile([P, E], U8, name="xb%d" % n)
             xb.append(xb_n)
-        for c in range(PASSES):
-            cols = slice(K_PASS * c, K_PASS * (c + 1))
-            nc.sync.dma_start(out=xb[0][:, cols], in_=x_bytes[0, 0, :, cols])
+
+        def load_x(n, c0, c1):
+            nc.sync.dma_start(out=xb[n][:, c0:c1], in_=x_bytes[n, 0, :, c0:c1])
+
+        sb = const.tile([P, E], F32, name="sb")
+        scale_row = x_scale.rearrange("a b c k -> (a b c k)")
+
+        def load_sb(h):
+            cols = slice(HALF * h, HALF * (h + 1))
+            nc.sync.dma_start(out=sb[:, cols], in_=scale_row[cols].partition_broadcast(P))
+
+        load_x(0, 0, 512)
+        load_x(0, 512, 1024)
+        load_x(0, 1024, 1536)
+        load_x(0, 1536, 2048)
+        load_x(3, 0, HALF)
+        load_x(3, HALF, E)
+        load_x(1, 0, E)
+        load_sb(0)
+        load_x(2, 0, E)
+        load_sb(1)
+        load_x(4, 0, E)
         w_sb = const.tile([P, E], BF16, name="w_sb")
-        nc.sync.dma_start(out=xb[1][:], in_=x_bytes[1, 0, :, :])
         nc.sync.dma_start(out=w_sb[:], in_=Wq[:, :])
-        nc.sync.dma_start(out=xb[2][:], in_=x_bytes[2, 0, :, :])
+        load_x(5, 0, E)
         d_sb = const.tile([P, L], BF16, name="d_sb")
         nc.sync.dma_start(out=d_sb[:], in_=decay_mask.rearrange("o q k -> (o q) k"))
         kv_sb = const.tile([P, NS, L], BF16, name="kv_sb")
         nc.sync.dma_start(out=kv_sb[:], in_=kv.rearrange("n o l k -> l (n o) k"))
         bq_col = const.tile([P, 1], BF16, name="bq_col")
         nc.sync.dma_start(out=bq_col[:], in_=bq.rearrange("(p o) -> p o", o=1))
-        for n in range(3, NS):
-            nc.sync.dma_start(out=xb[n][:], in_=x_bytes[n, 0, :, :])
+        for n in range(6, NS):
+            load_x(n, 0, E)
 
         one = const.tile([P, 1], F32, name="one")
         nc.gpsimd.memset(one[:], 1.0)
@@ -86,8 +105,9 @@ def tile_parallelretention_pb_kernel(tc, x_bytes, x_scale, Wq, bq, kv, decay_mas
         g_sb = const.tile([P, NS * L], F32, name="g_sb")
 
         xs = {}
+        xc = {}
         banks = {}
-        grouped = {}
+        grp = {}
         codes = {}
         scales = {}
         q_bank = {}
@@ -99,39 +119,74 @@ def tile_parallelretention_pb_kernel(tc, x_bytes, x_scale, Wq, bq, kv, decay_mas
             for n in group:
                 group_of[n] = gi
 
-        def widen(n):
-            xs_n = work.tile([P, E], BF16, name="xs")
-            xs[n] = xs_n
-            for g0, g1 in pieces(n):
-                cols = slice(K_PASS * g0, K_PASS * g1)
-                nc.scalar.copy(out=xs_n[:, cols], in_=xb[n][:, cols].bitcast(FP8))
-
-        def turn(words, parts):
-            tiles = []
-            for g0, g1 in parts:
-                np_ = g1 - g0
-                xt = psum.tile([P, 512], F32, tag="xt", bufs=3, name="xt")
-                for gi in range(np_):
-                    for u in range(2):
-                        s = np_ * u + gi
-                        lo = 256 * (g0 + gi)
-                        nc.tensor.transpose(
-                            out=xt[:, 128 * s : 128 * (s + 1)],
-                            in_=words[:, lo + u : lo + 256 : 2],
-                            identity=ident32[:],
-                        )
-                tiles.append(xt)
-            return tiles
-
-        def scale_out(n, i):
+        def cast(n, i):
             if i == 0:
-                grouped_n = work.tile([P, E], BF16, name="grouped", align_bytes=64)
-                grouped[n] = grouped_n
+                xs_n = work.tile([P, E], BF16, name="xs", bufs=4)
+                xs[n] = xs_n
+            g0, g1 = pieces(n)[i]
+            cols = slice(K_PASS * g0, K_PASS * g1)
+            nc.scalar.copy(out=xs[n][:, cols], in_=xb[n][:, cols].bitcast(FP8))
+
+        def vcast(n, c0, c1):
+            if c0 == 0:
+                xc_n = work.tile([P, E], BF16, name="xc", bufs=2)
+                xc[n] = xc_n
+            nc.vector.tensor_copy(out=xc[n][:, c0:c1], in_=xb[n][:, c0:c1].bitcast(FP8))
+
+        def vcast_c(n):
+            xs_n = work.tile([P, E], BF16, name="xs", bufs=4)
+            xs[n] = xs_n
+            nc.vector.tensor_copy(out=xs_n[:], in_=xb[n][:].bitcast(FP8))
+
+        def vcast_piece(n, i):
+            g0, g1 = pieces(n)[i]
+            cols = slice(K_PASS * g0, K_PASS * g1)
+            nc.vector.tensor_copy(out=xs[n][:, cols], in_=xb[n][:, cols].bitcast(FP8))
+
+        def scast_g(n, c0, c1):
+            nc.scalar.copy(out=xc[n][:, c0:c1], in_=xb[n][:, c0:c1].bitcast(FP8))
+
+        def gmul(n, h):
+            if h == 0:
+                xg_n = work.tile([P, E], BF16, name="xg", bufs=2)
+                xs[n] = xg_n
+            cols = slice(HALF * h, HALF * (h + 1))
+            nc.gpsimd.tensor_tensor(out=xs[n][:, cols], in0=xc[n][:, cols], in1=sb[:, cols], op=ALU.mult)
+
+        def turn_words(words, part, tag, bufs):
+            g0, g1 = part
+            np_ = g1 - g0
+            xt = psum.tile([P, 512], F32, tag=tag, bufs=bufs, name="xt")
+            for gi in range(np_):
+                for u in range(2):
+                    s = np_ * u + gi
+                    lo = 256 * (g0 + gi)
+                    nc.tensor.transpose(
+                        out=xt[:, 128 * s : 128 * (s + 1)],
+                        in_=words[:, lo + u : lo + 256 : 2],
+                        identity=ident32[:],
+                    )
+            return xt
+
+        def turn(n, i):
+            banks[(n, i)] = turn_words(xs[n][:].bitcast(F32), pieces(n)[i], "xt", 4)
+
+        def pair_tile(n):
+            pr = n // 2
+            if pr not in grp:
+                grp_pr = work.tile([P, 2 * E], BF16, name="grp", align_bytes=64)
+                grp[pr] = grp_pr
+            return grp[pr], E * (n % 2)
+
+        def so(n, i):
+            dst, base = pair_tile(n)
             g0, g1 = pieces(n)[i]
             np_ = g1 - g0
             nc.vector.tensor_tensor(
-                out=grouped[n][:, 512 * g0 : 512 * g1].rearrange("p (g r u e) -> p g r u e", g=np_, u=2, e=2),
-                in0=banks[n][i][:, 0 : 256 * np_].bitcast(BF16).rearrange(
+                out=dst[:, base + 512 * g0 : base + 512 * g1].rearrange(
+                    "p (g r u e) -> p g r u e", g=np_, u=2, e=2
+                ),
+                in0=banks[(n, i)][:, 0 : 256 * np_].bitcast(BF16).rearrange(
                     "p (u g r e) -> p g r u e", u=2, g=np_, e=2
                 ),
                 in1=sct[:, g0:g1, :].rearrange("p g (o u e) -> p g o u e", o=1, u=2).to_broadcast(
@@ -140,32 +195,49 @@ def tile_parallelretention_pb_kernel(tc, x_bytes, x_scale, Wq, bq, kv, decay_mas
                 op=ALU.mult,
             )
 
-        def quantize_x(n, g0, g1):
-            if g0 == 0:
-                codes_n = work.tile([P, E // 4], U32, name="codes", align_bytes=64)
-                scales_n = work.tile([P, E // 4], U8, name="scales", align_bytes=64)
-                codes[n] = codes_n
-                scales[n] = scales_n
-            nc.vector.quantize_mx(
-                out=codes[n][:, 128 * g0 : 128 * g1].bitcast(FP8X4),
-                scales=scales[n][:, 128 * g0 : 128 * g1],
-                in_=grouped[n][:, 512 * g0 : 512 * g1],
+        def words_out(dst, bank):
+            nc.scalar.copy(
+                out=dst.bitcast(F32).rearrange("p (g r u) -> p g r u", g=2, u=2),
+                in_=bank[:].rearrange("p (u g r) -> p g r u", u=2, g=2),
             )
 
-        def multiply(n):
+        def evac(n, i):
+            dst, base = pair_tile(n)
+            g0, g1 = pieces(n)[i]
+            words_out(dst[:, base + 512 * g0 : base + 512 * g1], banks[(n, i)])
+
+        def quant(pr, lo, hi):
+            if pr not in codes:
+                codes_pr = work.tile([P, E // 2], U32, name="codes", align_bytes=64)
+                scales_pr = work.tile([P, E // 2], U8, name="scales", align_bytes=64)
+                codes[pr] = codes_pr
+                scales[pr] = scales_pr
+            nc.vector.quantize_mx(
+                out=codes[pr][:, lo // 4 : hi // 4].bitcast(FP8X4),
+                scales=scales[pr][:, lo // 4 : hi // 4],
+                in_=grp[pr][:, lo:hi],
+            )
+
+        def mx(n):
             gi = group_of[n]
             j = n - GROUPS[gi][0]
-            if j == 0:
-                qp = psum.tile([P, 512], F32, tag="q", bufs=2, name="qp")
+            if gi not in q_bank:
+                if gi < LAST:
+                    qp = psum.tile([P, 512], F32, tag="q", bufs=1, name="qp")
+                else:
+                    qp = psum.tile([P, 512], F32, tag="xt", bufs=4, name="qp")
                 q_bank[gi] = qp
+            pr = n // 2
+            base = 512 * (n % 2)
             for g in range(PASSES):
                 gc = slice(128 * g, 128 * (g + 1))
+                xc_ = slice(base + 128 * g, base + 128 * (g + 1))
                 nc.tensor.matmul_mx(
                     out=q_bank[gi][:, 128 * j : 128 * (j + 1)],
                     lhsT=w_codes[:, gc].bitcast(FP8X4),
                     lhsT_scale=w_scales[:, gc],
-                    rhs=codes[n][:, gc].bitcast(FP8X4),
-                    rhs_scale=scales[n][:, gc],
+                    rhs=codes[pr][:, xc_].bitcast(FP8X4),
+                    rhs_scale=scales[pr][:, xc_],
                     start=(g == 0),
                     stop=(g == PASSES - 1),
                 )
@@ -176,7 +248,7 @@ def tile_parallelretention_pb_kernel(tc, x_bytes, x_scale, Wq, bq, kv, decay_mas
             w = 128 * m
             y = work.tile([P, 512], F32, name="y")
             ep[gi]["y"] = y
-            if gi < LAST:
+            if gi not in VECTOR_SUMS:
                 nc.vector.scalar_tensor_tensor(
                     out=y[:, 0:w],
                     in0=q_bank[gi][:, 0:w],
@@ -208,25 +280,46 @@ def tile_parallelretention_pb_kernel(tc, x_bytes, x_scale, Wq, bq, kv, decay_mas
                     out=yt[:, 128 * j : 128 * (j + 1)], in_=y[:, 128 * j : 128 * (j + 1)], identity=ident32[:]
                 )
 
-        def sums(gi):
+        def stat_bank(gi):
+            if gi < LAST:
+                st = psum.tile([P, 16], F32, tag="st", bufs=1, name="st")
+            else:
+                st = psum.tile([P, 16], F32, tag="xt", bufs=4, name="st")
+            ep[gi]["st"] = st
+
+        def colsum(gi):
             y = ep[gi]["y"]
-            s1 = small.tile([P, 4], F32, name="s1")
-            ep[gi]["s1"] = s1
+            stat_bank(gi)
             for j in range(len(GROUPS[gi])):
-                junk = work.tile([P, 128], F32, name="junk")
-                nc.scalar.activation(
-                    out=junk[:], in_=y[:, 128 * j : 128 * (j + 1)], func=ACT.Identity, accum_out=s1[:, j : j + 1]
+                nc.tensor.matmul(
+                    out=ep[gi]["st"][:, j : j + 1],
+                    lhsT=y[:, 128 * j : 128 * (j + 1)],
+                    rhs=one[:, 0:1],
+                    start=True,
+                    stop=True,
                 )
 
-        def mean_and_squares(gi):
+        def cs_copy(gi):
+            m = len(GROUPS[gi])
+            s1 = small.tile([P, 4], F32, name="s1")
+            ep[gi]["s1"] = s1
+            nc.scalar.copy(out=s1[:, 0:m], in_=ep[gi]["st"][:, 0:m])
+
+        def stats1(gi):
+            m = len(GROUPS[gi])
+            if gi in VECTOR_SUMS:
+                stat_bank(gi)
+            nc.tensor.matmul(
+                out=ep[gi]["st"][:, 4 : 4 + m], lhsT=neg_avg[:], rhs=ep[gi]["s1"][:, 0:m], start=True, stop=True
+            )
+
+        def nm_squares(gi):
             m = len(GROUPS[gi])
             y = ep[gi]["y"]
-            st = psum.tile([P, 8], F32, tag="st", bufs=1, name="st")
-            ep[gi]["st"] = st
-            nc.tensor.matmul(out=st[:, 0:m], lhsT=neg_avg[:], rhs=ep[gi]["s1"][:, 0:m], start=True, stop=True)
+            st = ep[gi]["st"]
             nm = small.tile([P, 4], F32, name="nm")
             ep[gi]["nm"] = nm
-            nc.scalar.copy(out=nm[:, 0:m], in_=st[:, 0:m])
+            nc.scalar.copy(out=nm[:, 0:m], in_=st[:, 4 : 4 + m])
             s2 = small.tile([P, 4], F32, name="s2")
             ep[gi]["s2"] = s2
             for j in range(m):
@@ -239,13 +332,17 @@ def tile_parallelretention_pb_kernel(tc, x_bytes, x_scale, Wq, bq, kv, decay_mas
                     accum_out=s2[:, j : j + 1],
                 )
 
-        def deviation(gi):
+        def stats2(gi):
             m = len(GROUPS[gi])
             st = ep[gi]["st"]
-            nc.tensor.matmul(out=st[:, 4 : 4 + m], lhsT=pos_avg[:], rhs=ep[gi]["s2"][:, 0:m], start=True, stop=True)
+            nc.tensor.matmul(out=st[:, 8 : 8 + m], lhsT=pos_avg[:], rhs=ep[gi]["s2"][:, 0:m], start=True, stop=True)
+
+        def sdev(gi):
+            m = len(GROUPS[gi])
+            st = ep[gi]["st"]
             sd = small.tile([P, 4], F32, name="sd")
             ep[gi]["sd"] = sd
-            nc.scalar.activation(out=sd[:, 0:m], in_=st[:, 4 : 4 + m], func=ACT.Sqrt, bias=eps[:, 0:1])
+            nc.scalar.activation(out=sd[:, 0:m], in_=st[:, 8 : 8 + m], func=ACT.Sqrt, bias=eps[:, 0:1])
 
         def factors(gi):
             m = len(GROUPS[gi])
@@ -281,75 +378,209 @@ def tile_parallelretention_pb_kernel(tc, x_bytes, x_scale, Wq, bq, kv, decay_mas
                     )
             nc.sync.dma_start(out=out[n0 : n0 + m].rearrange("n l q -> l n q"), in_=o[:, 0:m, :])
 
-        def stage(gi, k):
-            return k - (GROUPS[gi][-1] + 2)
+        def kv_turn(c):
+            kt = psum.tile([P, 512], BF16, tag="yt", bufs=2, name="kt")
+            kv_state["ps"] = kt
+            for j in range(4):
+                nc.tensor.transpose(
+                    out=kt[:, 128 * j : 128 * (j + 1)], in_=kv_sb[:, 4 * c + j, :], identity=ident16[:]
+                )
 
-        n_groups = len(GROUPS)
-        for k in range(-2, NS + 4):
-            for gi in range(n_groups):
-                if stage(gi, k) == 1:
-                    mean_and_squares(gi)
-            for c in range(4):
-                if k == KV_TICK[c] + 1:
-                    kv_t = work.tile([P, 512], BF16, name="kv_t")
-                    kv_state[c] = kv_t
-                    nc.scalar.copy(out=kv_t[:], in_=kv_state["ps"][:])
-            if k == 0:
-                for i, (g0, g1) in enumerate(pieces(1)):
-                    nc.scalar.copy(
-                        out=w_grouped[:, 512 * g0 : 512 * g1].bitcast(F32).rearrange(
-                            "p (g r u) -> p g r u", g=2, u=2
-                        ),
-                        in_=banks["w"][i][:].rearrange("p (u g r) -> p g r u", u=2, g=2),
-                    )
-            if 0 <= k + 2 < NS:
-                widen(k + 2)
-            if 0 <= k + 1 < NS:
-                banks[k + 1] = turn(xs[k + 1][:].bitcast(F32), pieces(k + 1))
-            if k == -1:
-                banks["w"] = turn(w_sb[:].bitcast(F32), pieces(1))
-            if 0 <= k < NS:
-                scale_out(k, 0)
-            if 0 <= k - 1 < NS - 1:
-                quantize_x(k - 1, 0, PASSES)
-            if k - 1 == NS - 1:
-                quantize_x(k - 1, 0, 2)
-                quantize_x(k - 1, 2, PASSES)
-            if k == 1:
-                nc.vector.quantize_mx(out=w_codes[:].bitcast(FP8X4), scales=w_scales[:], in_=w_grouped[:])
-            for gi in range(n_groups):
-                if stage(gi, k) == 0:
-                    product(gi)
-            for gi in range(n_groups):
-                if stage(gi, k) == 2:
-                    factors(gi)
-            if 0 <= k < NS:
-                for i in range(1, len(pieces(k))):
-                    scale_out(k, i)
-            if 0 <= k - 1 < NS:
-                multiply(k - 1)
-            for gi in range(n_groups):
-                if stage(gi, k) == 0:
-                    turn_back(gi)
-                    if gi < LAST:
-                        sums(gi)
-                if stage(gi, k) == 1:
-                    deviation(gi)
-                if stage(gi, k) == 2:
-                    finish(gi)
-            for c in range(4):
-                if k == KV_TICK[c] + 1:
-                    gp = psum.tile([P, 512], F32, tag="yt", bufs=2, name="gp")
-                    nc.tensor.matmul(out=gp[:], lhsT=d_t[:], rhs=kv_state[c][:], start=True, stop=True)
-                    nc.scalar.copy(out=g_sb[:, 512 * c : 512 * (c + 1)], in_=gp[:])
-                if k == KV_TICK[c]:
-                    kt = psum.tile([P, 512], BF16, tag="yt", bufs=2, name="kt")
-                    kv_state["ps"] = kt
-                    for j in range(4):
-                        nc.tensor.transpose(
-                            out=kt[:, 128 * j : 128 * (j + 1)], in_=kv_sb[:, 4 * c + j, :], identity=ident16[:]
-                        )
-            if k == 0:
-                dt_ps = psum.tile([P, 512], BF16, tag="yt", bufs=2, name="dt_ps")
-                nc.tensor.transpose(out=dt_ps[:, 0:P], in_=d_sb[:], identity=ident16[:])
-                nc.scalar.copy(out=d_t[:], in_=dt_ps[:, 0:P])
+        def kv_copy(c):
+            kv_t = work.tile([P, 512], BF16, name="kv_t")
+            kv_state[c] = kv_t
+            nc.scalar.copy(out=kv_t[:], in_=kv_state["ps"][:])
+
+        def g_matmul(c):
+            gp = psum.tile([P, 512], F32, tag="yt", bufs=2, name="gp")
+            kv_state["gp"] = gp
+            nc.tensor.matmul(out=gp[:], lhsT=d_t[:], rhs=kv_state[c][:], start=True, stop=True)
+
+        def g_copy(c):
+            nc.scalar.copy(out=g_sb[:, 512 * c : 512 * (c + 1)], in_=kv_state["gp"][:])
+
+        def weights_turn(h):
+            banks[("w", h)] = turn_words(w_sb[:].bitcast(F32), (2 * h, 2 * h + 2), "yt", 2)
+
+        def weights_out(h):
+            words_out(w_grouped[:, HALF * h : HALF * (h + 1)], banks[("w", h)])
+
+        def decay_turn():
+            dt_ps = psum.tile([P, 512], BF16, tag="yt", bufs=2, name="dt_ps")
+            kv_state["dt"] = dt_ps
+            nc.tensor.transpose(out=dt_ps[:, 0:P], in_=d_sb[:], identity=ident16[:])
+
+        def decay_copy():
+            nc.scalar.copy(out=d_t[:], in_=kv_state["dt"][:, 0:P])
+
+        cast(0, 0)
+        vcast_piece(0, 1)
+        cast(0, 2)
+        vcast_piece(0, 3)
+        turn(0, 0)
+        turn(0, 1)
+        vcast(3, 0, HALF)
+        turn(0, 2)
+        vcast(3, HALF, E)
+        so(0, 0)
+        gmul(3, 0)
+        turn(0, 3)
+        cast(1, 0)
+        so(0, 1)
+        turn(1, 0)
+        cast(1, 1)
+        so(0, 2)
+        turn(1, 1)
+        so(0, 3)
+        gmul(3, 1)
+        cast(2, 0)
+        so(1, 0)
+        turn(2, 0)
+        cast(2, 1)
+        so(1, 1)
+        turn(2, 1)
+        cast(4, 0)
+        so(2, 0)
+        turn(3, 0)
+        evac(3, 0)
+        cast(4, 1)
+        so(2, 1)
+        turn(3, 1)
+        evac(3, 1)
+        weights_turn(0)
+        weights_turn(1)
+        weights_out(0)
+        weights_out(1)
+        quant(0, 0, 2 * E)
+        vcast_c(6)
+        turn(4, 0)
+        turn(4, 1)
+        cast(5, 0)
+        decay_turn()
+        decay_copy()
+        kv_turn(0)
+        kv_copy(0)
+        quant(1, 0, 2 * E)
+        turn(5, 0)
+        cast(5, 1)
+        g_matmul(0)
+        g_copy(0)
+        turn(5, 1)
+        nc.vector.quantize_mx(out=w_codes[:].bitcast(FP8X4), scales=w_scales[:], in_=w_grouped[:])
+        mx(0)
+        mx(1)
+        vcast(7, 0, E)
+        mx(2)
+        mx(3)
+
+        def members(j):
+            if j < 3:
+                return 4 * j, 4 * j + 1, 4 * j + 2, 4 * j + 3
+            return 12, 13, 15, 14
+
+        for j in (1, 2):
+            a, b, d, c = members(j)
+            a2, b2, d2, c2 = members(j + 1)
+            g = j - 1
+            so(a, 0)
+            gmul(c, 0)
+            cast(a2, 0)
+            kv_turn(j)
+            so(a, 1)
+            cast(a2, 1)
+            turn(d, 0)
+            product(g)
+            kv_copy(j)
+            gmul(c, 1)
+            turn(d, 1)
+            so(b, 0)
+            cast(b2, 0)
+            colsum(g)
+            turn_back(g)
+            cs_copy(g)
+            so(b, 1)
+            turn(c, 0)
+            stats1(g)
+            cast(b2, 1)
+            g_matmul(j)
+            evac(c, 0)
+            so(d, 0)
+            nm_squares(g)
+            turn(c, 1)
+            evac(c, 1)
+            so(d, 1)
+            turn(a2, 0)
+            stats2(g)
+            g_copy(j)
+            sdev(g)
+            turn(a2, 1)
+            quant(a // 2, 0, 2 * E)
+            cast(d2, 0)
+            turn(b2, 0)
+            turn(b2, 1)
+            quant(d // 2, 0, 2 * E)
+            cast(d2, 1)
+            mx(a)
+            mx(b)
+            factors(g)
+            if j == 1:
+                vcast(c2, 0, E)
+            else:
+                vcast(c2, 0, HALF)
+                scast_g(c2, HALF, E)
+            mx(d)
+            mx(c)
+            finish(g)
+
+        so(12, 0)
+        gmul(14, 0)
+        kv_turn(3)
+        so(12, 1)
+        turn(15, 0)
+        product(2)
+        kv_copy(3)
+        gmul(14, 1)
+        turn(15, 1)
+        so(13, 0)
+        colsum(2)
+        turn_back(2)
+        cs_copy(2)
+        so(13, 1)
+        turn(14, 0)
+        stats1(2)
+        g_matmul(3)
+        evac(14, 0)
+        nm_squares(2)
+        turn(14, 1)
+        evac(14, 1)
+        quant(6, 0, 2 * E)
+        stats2(2)
+        g_copy(3)
+        sdev(2)
+        so(15, 0)
+        mx(12)
+        mx(13)
+        quant(7, 0, E)
+        so(15, 1)
+        mx(14)
+        quant(7, E, E + HALF)
+        quant(7, E + HALF, 2 * E)
+        mx(15)
+        factors(2)
+        finish(2)
+        product(3)
+        turn_back(3)
+        stats1(3)
+        nm_squares(3)
+        product(4)
+        turn_back(4)
+        stats1(4)
+        nm_squares(4)
+        stats2(3)
+        sdev(3)
+        stats2(4)
+        sdev(4)
+        factors(3)
+        finish(3)
+        factors(4)
+        finish(4)

@@ -144,14 +144,22 @@ def tile_parallelretention_pb_kernel(tc, x_bytes, x_scale, Wq, bq, kv, decay_mas
             nc.vector.tensor_copy(out=xs[n][:, cols], in_=xb[n][:, cols].bitcast(FP8))
 
         def scast_g(n, c0, c1):
+            if c0 == 0:
+                xc_n = work.tile([P, E], BF16, name="xc", bufs=2)
+                xc[n] = xc_n
             nc.scalar.copy(out=xc[n][:, c0:c1], in_=xb[n][:, c0:c1].bitcast(FP8))
 
-        def gmul(n, h):
-            if h == 0:
+        def gcast(n, c0, c1):
+            if c0 == 0:
+                xc_n = work.tile([P, E], BF16, name="xc", bufs=2)
+                xc[n] = xc_n
+            nc.gpsimd.tensor_copy(out=xc[n][:, c0:c1], in_=xb[n][:, c0:c1].bitcast(FP8))
+
+        def gmul(n, c0, c1):
+            if c0 == 0:
                 xg_n = work.tile([P, E], BF16, name="xg", bufs=2)
                 xs[n] = xg_n
-            cols = slice(HALF * h, HALF * (h + 1))
-            nc.gpsimd.tensor_tensor(out=xs[n][:, cols], in0=xc[n][:, cols], in1=sb[:, cols], op=ALU.mult)
+            nc.gpsimd.tensor_tensor(out=xs[n][:, c0:c1], in0=xc[n][:, c0:c1], in1=sb[:, c0:c1], op=ALU.mult)
 
         def turn_words(words, part, tag, bufs):
             g0, g1 = part
@@ -351,7 +359,9 @@ def tile_parallelretention_pb_kernel(tc, x_bytes, x_scale, Wq, bq, kv, decay_mas
             ep[gi]["rs"] = rs
             ep[gi]["nr"] = nr
             nc.vector.reciprocal(out=rs[:, 0:m], in_=ep[gi]["sd"][:, 0:m])
-            if gi < LAST:
+            if gi < 2:
+                nc.gpsimd.tensor_tensor(out=nr[:, 0:m], in0=ep[gi]["nm"][:, 0:m], in1=rs[:, 0:m], op=ALU.mult)
+            elif gi < LAST:
                 nc.vector.tensor_tensor(out=nr[:, 0:m], in0=ep[gi]["nm"][:, 0:m], in1=rs[:, 0:m], op=ALU.mult)
 
         def finish(gi):
@@ -417,27 +427,26 @@ def tile_parallelretention_pb_kernel(tc, x_bytes, x_scale, Wq, bq, kv, decay_mas
         vcast_piece(0, 1)
         cast(0, 2)
         vcast_piece(0, 3)
+        gcast(3, 0, E)
         turn(0, 0)
         turn(0, 1)
-        vcast(3, 0, HALF)
         turn(0, 2)
-        vcast(3, HALF, E)
         so(0, 0)
-        gmul(3, 0)
         turn(0, 3)
         cast(1, 0)
         so(0, 1)
         turn(1, 0)
         cast(1, 1)
         so(0, 2)
+        gmul(3, 0, HALF)
         turn(1, 1)
         so(0, 3)
-        gmul(3, 1)
         cast(2, 0)
         so(1, 0)
         turn(2, 0)
         cast(2, 1)
         so(1, 1)
+        gmul(3, HALF, E)
         turn(2, 1)
         cast(4, 0)
         so(2, 0)
@@ -469,7 +478,7 @@ def tile_parallelretention_pb_kernel(tc, x_bytes, x_scale, Wq, bq, kv, decay_mas
         nc.vector.quantize_mx(out=w_codes[:].bitcast(FP8X4), scales=w_scales[:], in_=w_grouped[:])
         mx(0)
         mx(1)
-        vcast(7, 0, E)
+        vcast(7, 0, K_PASS)
         mx(2)
         mx(3)
 
@@ -478,12 +487,21 @@ def tile_parallelretention_pb_kernel(tc, x_bytes, x_scale, Wq, bq, kv, decay_mas
                 return 4 * j, 4 * j + 1, 4 * j + 2, 4 * j + 3
             return 12, 13, 15, 14
 
+        def gpsimd_road(c, token):
+            if token:
+                gmul(c, 0, K_PASS)
+                gcast(c, K_PASS, E)
+                gmul(c, K_PASS, HALF)
+            else:
+                gcast(c, 0, E)
+                gmul(c, 0, HALF)
+
         for j in (1, 2):
             a, b, d, c = members(j)
             a2, b2, d2, c2 = members(j + 1)
             g = j - 1
             so(a, 0)
-            gmul(c, 0)
+            gpsimd_road(c, j == 1)
             cast(a2, 0)
             kv_turn(j)
             so(a, 1)
@@ -491,7 +509,7 @@ def tile_parallelretention_pb_kernel(tc, x_bytes, x_scale, Wq, bq, kv, decay_mas
             turn(d, 0)
             product(g)
             kv_copy(j)
-            gmul(c, 1)
+            gmul(c, HALF, E)
             turn(d, 1)
             so(b, 0)
             cast(b2, 0)
@@ -515,44 +533,47 @@ def tile_parallelretention_pb_kernel(tc, x_bytes, x_scale, Wq, bq, kv, decay_mas
             sdev(g)
             turn(a2, 1)
             quant(a // 2, 0, 2 * E)
-            cast(d2, 0)
+            if j == 1:
+                cast(d2, 0)
+            else:
+                scast_g(c2, 0, HALF)
             turn(b2, 0)
             turn(b2, 1)
             quant(d // 2, 0, 2 * E)
-            cast(d2, 1)
+            if j == 1:
+                cast(d2, 1)
+            else:
+                scast_g(c2, HALF, E)
             mx(a)
             mx(b)
             factors(g)
-            if j == 1:
-                vcast(c2, 0, E)
-            else:
-                vcast(c2, 0, HALF)
-                scast_g(c2, HALF, E)
             mx(d)
             mx(c)
             finish(g)
 
         so(12, 0)
-        gmul(14, 0)
+        gmul(14, 0, HALF)
+        cast(15, 0)
         kv_turn(3)
         so(12, 1)
-        turn(15, 0)
-        product(2)
         kv_copy(3)
-        gmul(14, 1)
-        turn(15, 1)
+        product(2)
+        gmul(14, HALF, E)
+        turn(14, 0)
         so(13, 0)
         colsum(2)
         turn_back(2)
         cs_copy(2)
-        so(13, 1)
-        turn(14, 0)
+        evac(14, 0)
         stats1(2)
         g_matmul(3)
-        evac(14, 0)
+        turn(15, 0)
+        cast(15, 1)
+        so(13, 1)
         nm_squares(2)
         turn(14, 1)
         evac(14, 1)
+        turn(15, 1)
         quant(6, 0, 2 * E)
         stats2(2)
         g_copy(3)
@@ -569,15 +590,15 @@ def tile_parallelretention_pb_kernel(tc, x_bytes, x_scale, Wq, bq, kv, decay_mas
         factors(2)
         finish(2)
         product(3)
-        turn_back(3)
         stats1(3)
         nm_squares(3)
         product(4)
-        turn_back(4)
         stats1(4)
         nm_squares(4)
+        turn_back(3)
         stats2(3)
         sdev(3)
+        turn_back(4)
         stats2(4)
         sdev(4)
         factors(3)

@@ -64,12 +64,9 @@ def tile_parallelretention_pb_kernel(tc, x_bytes, x_scale, Wq, bq, kv, decay_mas
         load_x(0, 512, 1024)
         load_x(0, 1024, 1536)
         load_x(0, 1536, 2048)
-        load_x(3, 0, HALF)
-        load_x(3, HALF, E)
         load_x(1, 0, E)
-        load_sb(0)
         load_x(2, 0, E)
-        load_sb(1)
+        load_x(3, 0, E)
         load_x(4, 0, E)
         w_sb = const.tile([P, E], BF16, name="w_sb")
         nc.sync.dma_start(out=w_sb[:], in_=Wq[:, :])
@@ -80,7 +77,11 @@ def tile_parallelretention_pb_kernel(tc, x_bytes, x_scale, Wq, bq, kv, decay_mas
         nc.sync.dma_start(out=kv_sb[:], in_=kv.rearrange("n o l k -> l (n o) k"))
         bq_col = const.tile([P, 1], BF16, name="bq_col")
         nc.sync.dma_start(out=bq_col[:], in_=bq.rearrange("(p o) -> p o", o=1))
-        for n in range(6, NS):
+        load_x(6, 0, E)
+        load_x(7, 0, E)
+        load_sb(0)
+        load_sb(1)
+        for n in range(8, NS):
             load_x(n, 0, E)
 
         one = const.tile([P, 1], F32, name="one")
@@ -427,7 +428,6 @@ def tile_parallelretention_pb_kernel(tc, x_bytes, x_scale, Wq, bq, kv, decay_mas
         vcast_piece(0, 1)
         cast(0, 2)
         vcast_piece(0, 3)
-        gcast(3, 0, E)
         turn(0, 0)
         turn(0, 1)
         turn(0, 2)
@@ -438,7 +438,6 @@ def tile_parallelretention_pb_kernel(tc, x_bytes, x_scale, Wq, bq, kv, decay_mas
         turn(1, 0)
         cast(1, 1)
         so(0, 2)
-        gmul(3, 0, HALF)
         turn(1, 1)
         so(0, 3)
         cast(2, 0)
@@ -446,19 +445,20 @@ def tile_parallelretention_pb_kernel(tc, x_bytes, x_scale, Wq, bq, kv, decay_mas
         turn(2, 0)
         cast(2, 1)
         so(1, 1)
-        gmul(3, HALF, E)
         turn(2, 1)
-        cast(4, 0)
+        cast(3, 0)
         so(2, 0)
         turn(3, 0)
-        evac(3, 0)
-        cast(4, 1)
+        cast(3, 1)
         so(2, 1)
         turn(3, 1)
-        evac(3, 1)
+        cast(4, 0)
+        so(3, 0)
         weights_turn(0)
         weights_turn(1)
         weights_out(0)
+        cast(4, 1)
+        so(3, 1)
         weights_out(1)
         quant(0, 0, 2 * E)
         vcast_c(6)

@@ -67,18 +67,18 @@ def tile_parallelretention_pb_kernel(tc, x_bytes, x_scale, Wq, bq, kv, decay_mas
         load_x(1, 0, E)
         load_x(2, 0, E)
         load_x(3, 0, E)
+        load_x(5, 0, E)
         load_x(4, 0, E)
+        load_x(7, 0, E)
+        load_x(6, 0, E)
         w_sb = const.tile([P, E], BF16, name="w_sb")
         nc.sync.dma_start(out=w_sb[:], in_=Wq[:, :])
-        load_x(5, 0, E)
         d_sb = const.tile([P, L], BF16, name="d_sb")
         nc.sync.dma_start(out=d_sb[:], in_=decay_mask.rearrange("o q k -> (o q) k"))
         kv_sb = const.tile([P, NS, L], BF16, name="kv_sb")
         nc.sync.dma_start(out=kv_sb[:], in_=kv.rearrange("n o l k -> l (n o) k"))
         bq_col = const.tile([P, 1], BF16, name="bq_col")
         nc.sync.dma_start(out=bq_col[:], in_=bq.rearrange("(p o) -> p o", o=1))
-        load_x(6, 0, E)
-        load_x(7, 0, E)
         load_sb(0)
         load_sb(1)
         for n in range(8, NS):
@@ -129,7 +129,7 @@ def tile_parallelretention_pb_kernel(tc, x_bytes, x_scale, Wq, bq, kv, decay_mas
             nc.scalar.copy(out=xs[n][:, cols], in_=xb[n][:, cols].bitcast(FP8))
 
         def vcast(n, c0, c1):
-            if c0 == 0:
+            if n not in xc:
                 xc_n = work.tile([P, E], BF16, name="xc", bufs=2)
                 xc[n] = xc_n
             nc.vector.tensor_copy(out=xc[n][:, c0:c1], in_=xb[n][:, c0:c1].bitcast(FP8))
@@ -138,6 +138,11 @@ def tile_parallelretention_pb_kernel(tc, x_bytes, x_scale, Wq, bq, kv, decay_mas
             xs_n = work.tile([P, E], BF16, name="xs", bufs=4)
             xs[n] = xs_n
             nc.vector.tensor_copy(out=xs_n[:], in_=xb[n][:].bitcast(FP8))
+
+        def gcast_c(n):
+            xs_n = work.tile([P, E], BF16, name="xs", bufs=4)
+            xs[n] = xs_n
+            nc.gpsimd.tensor_copy(out=xs_n[:], in_=xb[n][:].bitcast(FP8))
 
         def vcast_piece(n, i):
             g0, g1 = pieces(n)[i]
@@ -151,7 +156,7 @@ def tile_parallelretention_pb_kernel(tc, x_bytes, x_scale, Wq, bq, kv, decay_mas
             nc.scalar.copy(out=xc[n][:, c0:c1], in_=xb[n][:, c0:c1].bitcast(FP8))
 
         def gcast(n, c0, c1):
-            if c0 == 0:
+            if n not in xc:
                 xc_n = work.tile([P, E], BF16, name="xc", bufs=2)
                 xc[n] = xc_n
             nc.gpsimd.tensor_copy(out=xc[n][:, c0:c1], in_=xb[n][:, c0:c1].bitcast(FP8))
@@ -282,7 +287,10 @@ def tile_parallelretention_pb_kernel(tc, x_bytes, x_scale, Wq, bq, kv, decay_mas
 
         def turn_back(gi):
             y = ep[gi]["y"]
-            yt = psum.tile([P, 512], F32, tag="yt", bufs=2, name="yt")
+            if gi < 3:
+                yt = psum.tile([P, 512], F32, tag="yt", bufs=2, name="yt")
+            else:
+                yt = psum.tile([P, 512], F32, tag="xt", bufs=4, name="yt")
             ep[gi]["yt"] = yt
             for j in range(len(GROUPS[gi])):
                 nc.tensor.transpose(
@@ -447,6 +455,9 @@ def tile_parallelretention_pb_kernel(tc, x_bytes, x_scale, Wq, bq, kv, decay_mas
         so(1, 1)
         turn(2, 1)
         cast(3, 0)
+        gcast_c(5)
+        gcast(7, K_PASS, E)
+        gcast_c(6)
         so(2, 0)
         turn(3, 0)
         cast(3, 1)
@@ -461,17 +472,14 @@ def tile_parallelretention_pb_kernel(tc, x_bytes, x_scale, Wq, bq, kv, decay_mas
         so(3, 1)
         weights_out(1)
         quant(0, 0, 2 * E)
-        vcast_c(6)
         turn(4, 0)
         turn(4, 1)
-        cast(5, 0)
         decay_turn()
         decay_copy()
         kv_turn(0)
         kv_copy(0)
         quant(1, 0, 2 * E)
         turn(5, 0)
-        cast(5, 1)
         g_matmul(0)
         g_copy(0)
         turn(5, 1)
@@ -490,10 +498,8 @@ def tile_parallelretention_pb_kernel(tc, x_bytes, x_scale, Wq, bq, kv, decay_mas
         def gpsimd_road(c, token):
             if token:
                 gmul(c, 0, K_PASS)
-                gcast(c, K_PASS, E)
                 gmul(c, K_PASS, HALF)
             else:
-                gcast(c, 0, E)
                 gmul(c, 0, HALF)
 
         for j in (1, 2):
@@ -507,11 +513,13 @@ def tile_parallelretention_pb_kernel(tc, x_bytes, x_scale, Wq, bq, kv, decay_mas
             so(a, 1)
             cast(a2, 1)
             turn(d, 0)
-            product(g)
             kv_copy(j)
             gmul(c, HALF, E)
+            if j == 1:
+                gcast(c2, 0, E)
             turn(d, 1)
             so(b, 0)
+            product(g)
             cast(b2, 0)
             colsum(g)
             turn_back(g)

@@ -297,6 +297,16 @@ def tile_parallelretention_pb_kernel(tc, x_bytes, x_scale, Wq, bq, kv, decay_mas
                     out=yt[:, 128 * j : 128 * (j + 1)], in_=y[:, 128 * j : 128 * (j + 1)], identity=ident32[:]
                 )
 
+        def sums(gi):
+            y = ep[gi]["y"]
+            s1 = small.tile([P, 4], F32, name="s1")
+            ep[gi]["s1"] = s1
+            for j in range(len(GROUPS[gi])):
+                junk = work.tile([P, 128], F32, name="junk")
+                nc.scalar.activation(
+                    out=junk[:], in_=y[:, 128 * j : 128 * (j + 1)], func=ACT.Identity, accum_out=s1[:, j : j + 1]
+                )
+
         def stat_bank(gi):
             if gi < LAST:
                 st = psum.tile([P, 16], F32, tag="st", bufs=1, name="st")
@@ -324,7 +334,7 @@ def tile_parallelretention_pb_kernel(tc, x_bytes, x_scale, Wq, bq, kv, decay_mas
 
         def stats1(gi):
             m = len(GROUPS[gi])
-            if gi in VECTOR_SUMS:
+            if "st" not in ep[gi]:
                 stat_bank(gi)
             nc.tensor.matmul(
                 out=ep[gi]["st"][:, 4 : 4 + m], lhsT=neg_avg[:], rhs=ep[gi]["s1"][:, 0:m], start=True, stop=True
@@ -348,6 +358,19 @@ def tile_parallelretention_pb_kernel(tc, x_bytes, x_scale, Wq, bq, kv, decay_mas
                     bias=nm[:, j : j + 1],
                     accum_out=s2[:, j : j + 1],
                 )
+
+        def vector_squares(gi):
+            y = ep[gi]["y"]
+            st = ep[gi]["st"]
+            s2 = small.tile([P, 4], F32, name="s2")
+            ep[gi]["s2"] = s2
+            yc = work.tile([P, 128], F32, name="yc")
+            nc.vector.tensor_scalar(out=yc[:], in0=y[:, 0:128], scalar1=st[:, 4:5], scalar2=None, op0=ALU.add)
+            junk = work.tile([P, 128], F32, name="junk")
+            nc.vector.scalar_tensor_tensor(
+                out=junk[:], in0=yc[:], scalar=1.0, in1=yc[:], op0=ALU.mult, op1=ALU.mult, accum_out=s2[:, 0:1]
+            )
+            ep[gi]["y"] = yc
 
         def stats2(gi):
             m = len(GROUPS[gi])
@@ -378,22 +401,27 @@ def tile_parallelretention_pb_kernel(tc, x_bytes, x_scale, Wq, bq, kv, decay_mas
             n0 = GROUPS[gi][0]
             o = work.tile([P, 4, 128], F32, name="o")
             for j in range(m):
-                if gi < LAST:
-                    nc.scalar.activation(
-                        out=o[:, j, :],
-                        in_=ep[gi]["yt"][:, 128 * j : 128 * (j + 1)],
-                        func=ACT.Identity,
-                        scale=ep[gi]["rs"][:, j : j + 1],
-                        bias=ep[gi]["nr"][:, j : j + 1],
+                yt_j = ep[gi]["yt"][:, 128 * j : 128 * (j + 1)]
+                if gi == LAST:
+                    nc.vector.tensor_scalar(
+                        out=o[:, j, :], in0=yt_j, scalar1=ep[gi]["rs"][:, j : j + 1], scalar2=None, op0=ALU.mult
                     )
-                else:
+                elif gi == LAST - 1 and j == m - 1:
                     nc.vector.tensor_scalar(
                         out=o[:, j, :],
-                        in0=ep[gi]["yt"][:, 128 * j : 128 * (j + 1)],
+                        in0=yt_j,
                         scalar1=ep[gi]["nm"][:, j : j + 1],
                         scalar2=ep[gi]["rs"][:, j : j + 1],
                         op0=ALU.add,
                         op1=ALU.mult,
+                    )
+                else:
+                    nc.scalar.activation(
+                        out=o[:, j, :],
+                        in_=yt_j,
+                        func=ACT.Identity,
+                        scale=ep[gi]["rs"][:, j : j + 1],
+                        bias=ep[gi]["nr"][:, j : j + 1],
                     )
             nc.sync.dma_start(out=out[n0 : n0 + m].rearrange("n l q -> l n q"), in_=o[:, 0:m, :])
 
@@ -511,47 +539,48 @@ def tile_parallelretention_pb_kernel(tc, x_bytes, x_scale, Wq, bq, kv, decay_mas
             cast(a2, 0)
             kv_turn(j)
             so(a, 1)
+            if j > 1:
+                product(g)
             cast(a2, 1)
             turn(d, 0)
             kv_copy(j)
             gmul(c, HALF, E)
-            if j == 1:
-                gcast(c2, 0, E)
+            gcast(c2, 0, E)
             turn(d, 1)
+            if j > 1:
+                colsum(g)
             so(b, 0)
-            product(g)
+            if j == 1:
+                product(g)
             cast(b2, 0)
-            colsum(g)
-            turn_back(g)
-            cs_copy(g)
-            so(b, 1)
             turn(c, 0)
-            stats1(g)
+            if j == 1:
+                colsum(g)
+            so(b, 1)
             cast(b2, 1)
-            g_matmul(j)
             evac(c, 0)
-            so(d, 0)
-            nm_squares(g)
+            cs_copy(g)
             turn(c, 1)
-            evac(c, 1)
-            so(d, 1)
-            turn(a2, 0)
-            stats2(g)
-            g_copy(j)
-            sdev(g)
-            turn(a2, 1)
-            quant(a // 2, 0, 2 * E)
+            turn_back(g)
+            stats1(g)
+            g_matmul(j)
+            so(d, 0)
             if j == 1:
                 cast(d2, 0)
-            else:
-                scast_g(c2, 0, HALF)
+            evac(c, 1)
+            nm_squares(g)
+            so(d, 1)
+            turn(a2, 0)
+            turn(a2, 1)
             turn(b2, 0)
-            turn(b2, 1)
-            quant(d // 2, 0, 2 * E)
+            stats2(g)
+            g_copy(j)
+            quant(a // 2, 0, 2 * E)
             if j == 1:
                 cast(d2, 1)
-            else:
-                scast_g(c2, HALF, E)
+            sdev(g)
+            turn(b2, 1)
+            quant(d // 2, 0, 2 * E)
             mx(a)
             mx(b)
             factors(g)
@@ -564,24 +593,23 @@ def tile_parallelretention_pb_kernel(tc, x_bytes, x_scale, Wq, bq, kv, decay_mas
         cast(15, 0)
         kv_turn(3)
         so(12, 1)
-        kv_copy(3)
+        cast(15, 1)
         product(2)
         gmul(14, HALF, E)
-        turn(14, 0)
-        so(13, 0)
-        colsum(2)
-        turn_back(2)
-        cs_copy(2)
-        evac(14, 0)
-        stats1(2)
-        g_matmul(3)
+        kv_copy(3)
         turn(15, 0)
-        cast(15, 1)
+        so(13, 0)
+        sums(2)
+        turn(14, 0)
+        g_matmul(3)
+        evac(14, 0)
+        turn_back(2)
+        stats1(2)
         so(13, 1)
         nm_squares(2)
+        turn(15, 1)
         turn(14, 1)
         evac(14, 1)
-        turn(15, 1)
         quant(6, 0, 2 * E)
         stats2(2)
         g_copy(3)
@@ -590,19 +618,19 @@ def tile_parallelretention_pb_kernel(tc, x_bytes, x_scale, Wq, bq, kv, decay_mas
         mx(12)
         mx(13)
         quant(7, 0, E)
+        factors(2)
+        finish(2)
         so(15, 1)
         mx(14)
         quant(7, E, E + HALF)
         quant(7, E + HALF, 2 * E)
         mx(15)
-        factors(2)
-        finish(2)
         product(3)
         stats1(3)
         nm_squares(3)
         product(4)
         stats1(4)
-        nm_squares(4)
+        vector_squares(4)
         turn_back(3)
         stats2(3)
         sdev(3)

@@ -60,6 +60,10 @@ def tile_parallelretention_pb_kernel(tc, x_bytes, x_scale, Wq, bq, kv, decay_mas
             cols = slice(HALF * h, HALF * (h + 1))
             nc.sync.dma_start(out=sb[:, cols], in_=scale_row[cols].partition_broadcast(P))
 
+        w_sb = const.tile([P, E], BF16, name="w_sb")
+        d_sb = const.tile([P, L], BF16, name="d_sb")
+        kv_sb = const.tile([P, NS, L], BF16, name="kv_sb")
+        bq_col = const.tile([P, 1], BF16, name="bq_col")
         load_x(0, 0, 512)
         load_x(0, 512, 1024)
         load_x(0, 1024, 1536)
@@ -71,18 +75,20 @@ def tile_parallelretention_pb_kernel(tc, x_bytes, x_scale, Wq, bq, kv, decay_mas
         load_x(4, 0, E)
         load_x(7, 0, E)
         load_x(6, 0, E)
-        w_sb = const.tile([P, E], BF16, name="w_sb")
         nc.sync.dma_start(out=w_sb[:], in_=Wq[:, :])
-        d_sb = const.tile([P, L], BF16, name="d_sb")
         nc.sync.dma_start(out=d_sb[:], in_=decay_mask.rearrange("o q k -> (o q) k"))
-        kv_sb = const.tile([P, NS, L], BF16, name="kv_sb")
         nc.sync.dma_start(out=kv_sb[:], in_=kv.rearrange("n o l k -> l (n o) k"))
-        bq_col = const.tile([P, 1], BF16, name="bq_col")
         nc.sync.dma_start(out=bq_col[:], in_=bq.rearrange("(p o) -> p o", o=1))
+        load_x(8, 0, E)
+        load_x(9, 0, E)
         load_sb(0)
         load_sb(1)
-        for n in range(8, NS):
-            load_x(n, 0, E)
+        load_x(10, 0, E)
+        load_x(11, 0, E)
+        load_x(12, 0, E)
+        load_x(13, 0, E)
+        load_x(14, 0, E)
+        load_x(15, 0, E)
 
         one = const.tile([P, 1], F32, name="one")
         nc.gpsimd.memset(one[:], 1.0)

@@ -93,7 +93,7 @@ def tile_parallelretention_pb_kernel(tc, x_bytes, x_scale, Wq, bq, kv, decay_mas
         one = const.tile([P, 1], F32, name="one")
         nc.gpsimd.memset(one[:], 1.0)
         warm = const.tile([P, 1], F32, name="warm")
-        nc.scalar.activation(out=warm[:], in_=one[:], func=ACT.Sqrt)
+        nc.scalar.activation(out=warm[:], in_=one[:], func=ACT.Abs_reciprocal_sqrt)
         ident32 = const.tile([P, P], F32, name="ident32")
         make_identity(nc, ident32[:])
         ident16 = const.tile([P, P], BF16, name="ident16")
@@ -386,21 +386,25 @@ def tile_parallelretention_pb_kernel(tc, x_bytes, x_scale, Wq, bq, kv, decay_mas
         def sdev(gi):
             m = len(GROUPS[gi])
             st = ep[gi]["st"]
-            sd = small.tile([P, 4], F32, name="sd")
-            ep[gi]["sd"] = sd
-            nc.scalar.activation(out=sd[:, 0:m], in_=st[:, 8 : 8 + m], func=ACT.Sqrt, bias=eps[:, 0:1])
+            rs = small.tile([P, 4], F32, name="rs")
+            ep[gi]["rs"] = rs
+            nc.scalar.activation(
+                out=rs[:, 0:m], in_=st[:, 8 : 8 + m], func=ACT.Abs_reciprocal_sqrt, bias=eps[:, 0:1]
+            )
 
         def factors(gi):
             m = len(GROUPS[gi])
-            rs = small.tile([P, 4], F32, name="rs")
-            nr = small.tile([P, 4], F32, name="nr")
-            ep[gi]["rs"] = rs
-            ep[gi]["nr"] = nr
-            nc.vector.reciprocal(out=rs[:, 0:m], in_=ep[gi]["sd"][:, 0:m])
-            if gi < 2:
-                nc.gpsimd.tensor_tensor(out=nr[:, 0:m], in0=ep[gi]["nm"][:, 0:m], in1=rs[:, 0:m], op=ALU.mult)
-            elif gi < LAST:
-                nc.vector.tensor_tensor(out=nr[:, 0:m], in0=ep[gi]["nm"][:, 0:m], in1=rs[:, 0:m], op=ALU.mult)
+            if gi < LAST:
+                nr = small.tile([P, 4], F32, name="nr")
+                ep[gi]["nr"] = nr
+                for j in range(m):
+                    if not (gi == LAST - 1 and j == m - 1):
+                        nc.scalar.activation(
+                            out=nr[:, j : j + 1],
+                            in_=ep[gi]["nm"][:, j : j + 1],
+                            func=ACT.Copy,
+                            scale=ep[gi]["rs"][:, j : j + 1],
+                        )
 
         def finish(gi):
             m = len(GROUPS[gi])
@@ -541,7 +545,7 @@ def tile_parallelretention_pb_kernel(tc, x_bytes, x_scale, Wq, bq, kv, decay_mas
             a2, b2, d2, c2 = members(j + 1)
             g = j - 1
             so(a, 0)
-            gpsimd_road(c, j == 1)
+            gpsimd_road(c, True)
             cast(a2, 0)
             kv_turn(j)
             so(a, 1)
@@ -551,7 +555,7 @@ def tile_parallelretention_pb_kernel(tc, x_bytes, x_scale, Wq, bq, kv, decay_mas
             turn(d, 0)
             kv_copy(j)
             gmul(c, HALF, E)
-            gcast(c2, 0, E)
+            gcast(c2, K_PASS, E)
             turn(d, 1)
             if j > 1:
                 colsum(g)
@@ -590,12 +594,13 @@ def tile_parallelretention_pb_kernel(tc, x_bytes, x_scale, Wq, bq, kv, decay_mas
             mx(a)
             mx(b)
             factors(g)
+            vcast(c2, 0, K_PASS)
             mx(d)
             mx(c)
             finish(g)
 
         so(12, 0)
-        gmul(14, 0, HALF)
+        gpsimd_road(14, True)
         cast(15, 0)
         kv_turn(3)
         so(12, 1)
@@ -616,11 +621,11 @@ def tile_parallelretention_pb_kernel(tc, x_bytes, x_scale, Wq, bq, kv, decay_mas
         turn(15, 1)
         turn(14, 1)
         evac(14, 1)
+        so(15, 0)
         quant(6, 0, 2 * E)
         stats2(2)
         g_copy(3)
         sdev(2)
-        so(15, 0)
         mx(12)
         mx(13)
         quant(7, 0, E)

@@ -70,11 +70,11 @@ def tile_parallelretention_pb_kernel(tc, x_bytes, x_scale, Wq, bq, kv, decay_mas
         load_x(0, 1536, 2048)
         load_x(1, 0, E)
         load_x(2, 0, E)
-        load_x(3, 0, E)
         load_x(5, 0, E)
-        load_x(4, 0, E)
+        load_x(3, 0, E)
         load_x(7, 0, E)
         load_x(6, 0, E)
+        load_x(4, 0, E)
         nc.sync.dma_start(out=w_sb[:], in_=Wq[:, :])
         nc.sync.dma_start(out=d_sb[:], in_=decay_mask.rearrange("o q k -> (o q) k"))
         nc.sync.dma_start(out=kv_sb[:], in_=kv.rearrange("n o l k -> l (n o) k"))
@@ -149,6 +149,11 @@ def tile_parallelretention_pb_kernel(tc, x_bytes, x_scale, Wq, bq, kv, decay_mas
             xs_n = work.tile([P, E], BF16, name="xs", bufs=4)
             xs[n] = xs_n
             nc.gpsimd.tensor_copy(out=xs_n[:], in_=xb[n][:].bitcast(FP8))
+
+        def vcast_first(n):
+            xs_n = work.tile([P, E], BF16, name="xs", bufs=4)
+            xs[n] = xs_n
+            vcast_piece(n, 0)
 
         def vcast_piece(n, i):
             g0, g1 = pieces(n)[i]
@@ -470,10 +475,10 @@ def tile_parallelretention_pb_kernel(tc, x_bytes, x_scale, Wq, bq, kv, decay_mas
         def decay_copy():
             nc.scalar.copy(out=d_t[:], in_=kv_state["dt"][:, 0:P])
 
-        cast(0, 0)
-        vcast_piece(0, 1)
-        cast(0, 2)
-        vcast_piece(0, 3)
+        vcast_first(0)
+        cast(0, 1)
+        vcast_piece(0, 2)
+        cast(0, 3)
         turn(0, 0)
         turn(0, 1)
         turn(0, 2)
@@ -643,9 +648,9 @@ def tile_parallelretention_pb_kernel(tc, x_bytes, x_scale, Wq, bq, kv, decay_mas
         stats1(4)
         vector_squares(4)
         turn_back(3)
+        turn_back(4)
         stats2(3)
         sdev(3)
-        turn_back(4)
         stats2(4)
         sdev(4)
         factors(3)

@@ -24,6 +24,7 @@ FLOPS = 2 * NS * L * E * QD + 2 * NS * L * QD * L
 
 GROUPS = [[0, 1, 2, 3], [4, 5, 6, 7], [8, 9, 10, 11], [12, 13, 14], [15]]
 VECTOR_SUMS = (3, 4)
+SHARED = {1: "swap_a", 3: "swap_b", 5: "swap_a"}
 LAST = len(GROUPS) - 1
 
 
@@ -69,10 +70,10 @@ def tile_parallelretention_pb_kernel(tc, x_bytes, x_scale, Wq, bq, kv, decay_mas
         load_x(0, 1024, 1536)
         load_x(0, 1536, 2048)
         load_x(1, 0, E)
-        load_x(2, 0, E)
         load_x(5, 0, E)
-        load_x(3, 0, E)
+        load_x(2, 0, E)
         load_x(7, 0, E)
+        load_x(3, 0, E)
         load_x(6, 0, E)
         load_x(4, 0, E)
         nc.sync.dma_start(out=w_sb[:], in_=Wq[:, :])
@@ -128,7 +129,7 @@ def tile_parallelretention_pb_kernel(tc, x_bytes, x_scale, Wq, bq, kv, decay_mas
 
         def cast(n, i):
             if i == 0:
-                xs_n = work.tile([P, E], BF16, name="xs", bufs=4)
+                xs_n = work.tile([P, E], BF16, name="xs", bufs=6)
                 xs[n] = xs_n
             g0, g1 = pieces(n)[i]
             cols = slice(K_PASS * g0, K_PASS * g1)
@@ -141,17 +142,17 @@ def tile_parallelretention_pb_kernel(tc, x_bytes, x_scale, Wq, bq, kv, decay_mas
             nc.vector.tensor_copy(out=xc[n][:, c0:c1], in_=xb[n][:, c0:c1].bitcast(FP8))
 
         def vcast_c(n):
-            xs_n = work.tile([P, E], BF16, name="xs", bufs=4)
+            xs_n = work.tile([P, E], BF16, name="xs", bufs=6)
             xs[n] = xs_n
             nc.vector.tensor_copy(out=xs_n[:], in_=xb[n][:].bitcast(FP8))
 
         def gcast_c(n):
-            xs_n = work.tile([P, E], BF16, name="xs", bufs=4)
+            xs_n = work.tile([P, E], BF16, name="xs", bufs=6)
             xs[n] = xs_n
             nc.gpsimd.tensor_copy(out=xs_n[:], in_=xb[n][:].bitcast(FP8))
 
         def vcast_first(n):
-            xs_n = work.tile([P, E], BF16, name="xs", bufs=4)
+            xs_n = work.tile([P, E], BF16, name="xs", bufs=6)
             xs[n] = xs_n
             vcast_piece(n, 0)
 
@@ -174,7 +175,7 @@ def tile_parallelretention_pb_kernel(tc, x_bytes, x_scale, Wq, bq, kv, decay_mas
 
         def gmul(n, c0, c1):
             if c0 == 0:
-                xg_n = work.tile([P, E], BF16, name="xg", bufs=2)
+                xg_n = held.tile([P, E], BF16, tag=SHARED[n // 2 - 2], name="xg", align_bytes=64)
                 xs[n] = xg_n
             nc.gpsimd.tensor_tensor(out=xs[n][:, c0:c1], in0=xc[n][:, c0:c1], in1=sb[:, c0:c1], op=ALU.mult)
 
@@ -199,7 +200,10 @@ def tile_parallelretention_pb_kernel(tc, x_bytes, x_scale, Wq, bq, kv, decay_mas
         def pair_tile(n):
             pr = n // 2
             if pr not in grp:
-                grp_pr = work.tile([P, 2 * E], BF16, name="grp", align_bytes=64)
+                if pr in SHARED:
+                    grp_pr = held.tile([P, 2 * E], BF16, tag=SHARED[pr], name="grp_s", align_bytes=64)
+                else:
+                    grp_pr = work.tile([P, 2 * E], BF16, name="grp", align_bytes=64)
                 grp[pr] = grp_pr
             return grp[pr], E * (n % 2)
 
@@ -499,7 +503,7 @@ def tile_parallelretention_pb_kernel(tc, x_bytes, x_scale, Wq, bq, kv, decay_mas
         turn(2, 1)
         cast(3, 0)
         gcast_c(5)
-        gcast(7, K_PASS, E)
+        gcast(7, 0, E)
         gcast_c(6)
         so(2, 0)
         turn(3, 0)
@@ -529,7 +533,6 @@ def tile_parallelretention_pb_kernel(tc, x_bytes, x_scale, Wq, bq, kv, decay_mas
         nc.vector.quantize_mx(out=w_codes[:].bitcast(FP8X4), scales=w_scales[:], in_=w_grouped[:])
         mx(0)
         mx(1)
-        vcast(7, 0, K_PASS)
         mx(2)
         mx(3)
 
@@ -550,7 +553,7 @@ def tile_parallelretention_pb_kernel(tc, x_bytes, x_scale, Wq, bq, kv, decay_mas
             a2, b2, d2, c2 = members(j + 1)
             g = j - 1
             so(a, 0)
-            gpsimd_road(c, True)
+            gpsimd_road(c, False)
             cast(a2, 0)
             kv_turn(j)
             so(a, 1)
@@ -560,7 +563,7 @@ def tile_parallelretention_pb_kernel(tc, x_bytes, x_scale, Wq, bq, kv, decay_mas
             turn(d, 0)
             kv_copy(j)
             gmul(c, HALF, E)
-            gcast(c2, K_PASS, E)
+            gcast(c2, 0, E)
             turn(d, 1)
             if j > 1:
                 colsum(g)
@@ -599,13 +602,12 @@ def tile_parallelretention_pb_kernel(tc, x_bytes, x_scale, Wq, bq, kv, decay_mas
             mx(a)
             mx(b)
             factors(g)
-            vcast(c2, 0, K_PASS)
             mx(d)
             mx(c)
             finish(g)
 
         so(12, 0)
-        gpsimd_road(14, True)
+        gpsimd_road(14, False)
         cast(15, 0)
         kv_turn(3)
         so(12, 1)

@@ -502,9 +502,7 @@ def tile_parallelretention_pb_kernel(tc, x_bytes, x_scale, Wq, bq, kv, decay_mas
         so(1, 1)
         turn(2, 1)
         cast(3, 0)
-        gcast_c(5)
         gcast(7, 0, E)
-        gcast_c(6)
         so(2, 0)
         turn(3, 0)
         cast(3, 1)
@@ -518,6 +516,8 @@ def tile_parallelretention_pb_kernel(tc, x_bytes, x_scale, Wq, bq, kv, decay_mas
         cast(4, 1)
         so(3, 1)
         weights_out(1)
+        cast(5, 0)
+        cast(5, 1)
         quant(0, 0, 2 * E)
         turn(4, 0)
         turn(4, 1)
@@ -529,6 +529,8 @@ def tile_parallelretention_pb_kernel(tc, x_bytes, x_scale, Wq, bq, kv, decay_mas
         turn(5, 0)
         g_matmul(0)
         g_copy(0)
+        cast(6, 0)
+        cast(6, 1)
         turn(5, 1)
         nc.vector.quantize_mx(out=w_codes[:].bitcast(FP8X4), scales=w_scales[:], in_=w_grouped[:])
         mx(0)

@@ -70,12 +70,12 @@ def tile_parallelretention_pb_kernel(tc, x_bytes, x_scale, Wq, bq, kv, decay_mas
         load_x(0, 1024, 1536)
         load_x(0, 1536, 2048)
         load_x(1, 0, E)
-        load_x(5, 0, E)
-        load_x(2, 0, E)
         load_x(7, 0, E)
         load_x(3, 0, E)
-        load_x(6, 0, E)
+        load_x(2, 0, E)
         load_x(4, 0, E)
+        load_x(5, 0, E)
+        load_x(6, 0, E)
         nc.sync.dma_start(out=w_sb[:], in_=Wq[:, :])
         nc.sync.dma_start(out=d_sb[:], in_=decay_mask.rearrange("o q k -> (o q) k"))
         nc.sync.dma_start(out=kv_sb[:], in_=kv.rearrange("n o l k -> l (n o) k"))
@@ -114,6 +114,7 @@ def tile_parallelretention_pb_kernel(tc, x_bytes, x_scale, Wq, bq, kv, decay_mas
 
         xs = {}
         xc = {}
+        xw = {}
         banks = {}
         grp = {}
         codes = {}
@@ -128,7 +129,7 @@ def tile_parallelretention_pb_kernel(tc, x_bytes, x_scale, Wq, bq, kv, decay_mas
                 group_of[n] = gi
 
         def cast(n, i):
-            if i == 0:
+            if n not in xs:
                 xs_n = work.tile([P, E], BF16, name="xs", bufs=6)
                 xs[n] = xs_n
             g0, g1 = pieces(n)[i]
@@ -234,6 +235,23 @@ def tile_parallelretention_pb_kernel(tc, x_bytes, x_scale, Wq, bq, kv, decay_mas
             dst, base = pair_tile(n)
             g0, g1 = pieces(n)[i]
             words_out(dst[:, base + 512 * g0 : base + 512 * g1], banks[(n, i)])
+
+        def evac_w(n, i):
+            if n not in xw:
+                xw_n = work.tile([P, E], BF16, name="xw", bufs=2)
+                xw[n] = xw_n
+            g0, g1 = pieces(n)[i]
+            words_out(xw[n][:, 512 * g0 : 512 * g1], banks[(n, i)])
+
+        def gmul_w(n, g0, g1):
+            dst, base = pair_tile(n)
+            np_ = g1 - g0
+            nc.gpsimd.tensor_tensor(
+                out=dst[:, base + 512 * g0 : base + 512 * g1].rearrange("p (g r t) -> p g r t", g=np_, t=4),
+                in0=xw[n][:, 512 * g0 : 512 * g1].rearrange("p (g r t) -> p g r t", g=np_, t=4),
+                in1=sct[:, g0:g1, :].rearrange("p g (o t) -> p g o t", o=1).to_broadcast([P, np_, 128, 4]),
+                op=ALU.mult,
+            )
 
         def quant(pr, lo, hi):
             if pr not in codes:
@@ -492,29 +510,30 @@ def tile_parallelretention_pb_kernel(tc, x_bytes, x_scale, Wq, bq, kv, decay_mas
         so(0, 1)
         turn(1, 0)
         cast(1, 1)
+        gcast(7, 0, E)
         so(0, 2)
         turn(1, 1)
+        cast(3, 1)
         so(0, 3)
+        turn(3, 1)
         cast(2, 0)
+        evac_w(3, 1)
         so(1, 0)
         turn(2, 0)
         cast(2, 1)
+        gmul_w(3, 2, 4)
         so(1, 1)
         turn(2, 1)
         cast(3, 0)
-        gcast(7, 0, E)
         so(2, 0)
         turn(3, 0)
-        cast(3, 1)
-        so(2, 1)
-        turn(3, 1)
         cast(4, 0)
-        so(3, 0)
+        so(2, 1)
         weights_turn(0)
         weights_turn(1)
         weights_out(0)
         cast(4, 1)
-        so(3, 1)
+        so(3, 0)
         weights_out(1)
         cast(5, 0)
         cast(5, 1)

from contextlib import ExitStack

import concourse.mybir as mybir
from concourse.masks import make_identity

F32 = mybir.dt.float32
BF16 = mybir.dt.bfloat16
U32 = mybir.dt.uint32
U8 = mybir.dt.uint8
FP8 = mybir.dt.float8_e4m3fn
FP8X4 = mybir.dt.float8_e4m3fn_x4
ALU = mybir.AluOpType
ACT = mybir.ActivationFunctionType

NS, L, E, QD = 16, 128, 2048, 128
P = 128
K_PASS = 512
PASSES = E // K_PASS
HALF = E // 2
EPS = 1e-5
COUNT = L * QD

FLOPS = 2 * NS * L * E * QD + 2 * NS * L * QD * L

GROUPS = [[0, 1, 2, 3], [4, 5, 6, 7], [8, 9, 10, 11], [12, 13, 14], [15]]
VECTOR_SUMS = (3, 4)
SHARED = {1: "swap_a", 3: "swap_b", 5: "swap_a"}
LAST = len(GROUPS) - 1


def pieces(n):
    if n == 0:
        return [(g, g + 1) for g in range(PASSES)]
    return [(0, 2), (2, 4)]


def tile_parallelretention_pb_kernel(tc, x_bytes, x_scale, Wq, bq, kv, decay_mask, out):
    nc = tc.nc
    with ExitStack() as ctx:
        const = ctx.enter_context(tc.tile_pool(name="const", bufs=1))
        held = ctx.enter_context(tc.tile_pool(name="held", bufs=1))
        work = ctx.enter_context(tc.tile_pool(name="work", bufs=3))
        small = ctx.enter_context(tc.tile_pool(name="small", bufs=2))
        psum = ctx.enter_context(tc.psum_pool(name="psum", bufs=1))
        ctx.enter_context(tc.manual_schedule())

        sct = const.tile([P, PASSES, 4], F32, name="sct")
        nc.scalar.dma_start(out=sct[:], in_=x_scale.rearrange("a b c (g p t) -> p (a b c g) t", p=P, t=4))
        xb = []
        for n in range(NS):
            xb_n = held.tile([P, E], U8, name="xb%d" % n)
            xb.append(xb_n)

        def load_x(n, c0, c1):
            nc.sync.dma_start(out=xb[n][:, c0:c1], in_=x_bytes[n, 0, :, c0:c1])

        sb = const.tile([P, E], F32, name="sb")
        scale_row = x_scale.rearrange("a b c k -> (a b c k)")

        def load_sb(h):
            cols = slice(HALF * h, HALF * (h + 1))
            nc.sync.dma_start(out=sb[:, cols], in_=scale_row[cols].partition_broadcast(P))

        w_sb = const.tile([P, E], BF16, name="w_sb")
        d_sb = const.tile([P, L], BF16, name="d_sb")
        kv_sb = const.tile([P, NS, L], BF16, name="kv_sb")
        bq_col = const.tile([P, 1], BF16, name="bq_col")
        load_x(0, 0, 512)
        load_x(0, 512, 1024)
        load_x(0, 1024, 1536)
        load_x(0, 1536, 2048)
        load_x(1, 0, E)
        load_x(7, 0, E)
        load_x(3, 0, E)
        load_x(2, 0, E)
        load_x(4, 0, E)
        load_x(5, 0, E)
        load_x(6, 0, E)
        nc.sync.dma_start(out=w_sb[:], in_=Wq[:, :])
        nc.sync.dma_start(out=d_sb[:], in_=decay_mask.rearrange("o q k -> (o q) k"))
        nc.sync.dma_start(out=kv_sb[:], in_=kv.rearrange("n o l k -> l (n o) k"))
        nc.sync.dma_start(out=bq_col[:], in_=bq.rearrange("(p o) -> p o", o=1))
        load_x(8, 0, E)
        load_x(9, 0, E)
        load_sb(0)
        load_sb(1)
        load_x(10, 0, E)
        load_x(11, 0, E)
        load_x(12, 0, E)
        load_x(13, 0, E)
        load_x(14, 0, E)
        load_x(15, 0, E)

        one = const.tile([P, 1], F32, name="one")
        nc.gpsimd.memset(one[:], 1.0)
        warm = const.tile([P, 1], F32, name="warm")
        nc.scalar.activation(out=warm[:], in_=one[:], func=ACT.Abs_reciprocal_sqrt)
        ident32 = const.tile([P, P], F32, name="ident32")
        make_identity(nc, ident32[:])
        ident16 = const.tile([P, P], BF16, name="ident16")
        make_identity(nc, ident16[:])
        neg_avg = const.tile([P, P], F32, name="neg_avg")
        nc.gpsimd.memset(neg_avg[:], -1.0 / COUNT)
        pos_avg = const.tile([P, P], F32, name="pos_avg")
        nc.gpsimd.memset(pos_avg[:], 1.0 / COUNT)
        eps = const.tile([P, 1], F32, name="eps")
        nc.gpsimd.memset(eps[:], EPS)

        w_grouped = const.tile([P, E], BF16, name="w_grouped", align_bytes=64)
        w_codes = const.tile([P, E // 4], U32, name="w_codes", align_bytes=64)
        w_scales = const.tile([P, E // 4], U8, name="w_scales", align_bytes=64)
        d_t = const.tile([P, P], BF16, name="d_t")
        g_sb = const.tile([P, NS * L], F32, name="g_sb")

        xs = {}
        xc = {}
        xw = {}
        banks = {}
        grp = {}
        codes = {}
        scales = {}
        q_bank = {}
        ep = {}
        kv_state = {}
        group_of = {}
        for gi, group in enumerate(GROUPS):
            ep[gi] = {}
            for n in group:
                group_of[n] = gi

        def cast(n, i):
            if n not in xs:
                xs_n = work.tile([P, E], BF16, name="xs", bufs=6)
                xs[n] = xs_n
            g0, g1 = pieces(n)[i]
            cols = slice(K_PASS * g0, K_PASS * g1)
            nc.scalar.copy(out=xs[n][:, cols], in_=xb[n][:, cols].bitcast(FP8))

        def vcast(n, c0, c1):
            if n not in xc:
                xc_n = work.tile([P, E], BF16, name="xc", bufs=2)
                xc[n] = xc_n
            nc.vector.tensor_copy(out=xc[n][:, c0:c1], in_=xb[n][:, c0:c1].bitcast(FP8))

        def vcast_c(n):
            xs_n = work.tile([P, E], BF16, name="xs", bufs=6)
            xs[n] = xs_n
            nc.vector.tensor_copy(out=xs_n[:], in_=xb[n][:].bitcast(FP8))

        def gcast_c(n):
            xs_n = work.tile([P, E], BF16, name="xs", bufs=6)
            xs[n] = xs_n
            nc.gpsimd.tensor_copy(out=xs_n[:], in_=xb[n][:].bitcast(FP8))

        def vcast_first(n):
            xs_n = work.tile([P, E], BF16, name="xs", bufs=6)
            xs[n] = xs_n
            vcast_piece(n, 0)

        def vcast_piece(n, i):
            g0, g1 = pieces(n)[i]
            cols = slice(K_PASS * g0, K_PASS * g1)
            nc.vector.tensor_copy(out=xs[n][:, cols], in_=xb[n][:, cols].bitcast(FP8))

        def scast_g(n, c0, c1):
            if c0 == 0:
                xc_n = work.tile([P, E], BF16, name="xc", bufs=2)
                xc[n] = xc_n
            nc.scalar.copy(out=xc[n][:, c0:c1], in_=xb[n][:, c0:c1].bitcast(FP8))

        def gcast(n, c0, c1):
            if n not in xc:
                xc_n = work.tile([P, E], BF16, name="xc", bufs=2)
                xc[n] = xc_n
            nc.gpsimd.tensor_copy(out=xc[n][:, c0:c1], in_=xb[n][:, c0:c1].bitcast(FP8))

        def gmul(n, c0, c1):
            if c0 == 0:
                xg_n = held.tile([P, E], BF16, tag=SHARED[n // 2 - 2], name="xg", align_bytes=64)
                xs[n] = xg_n
            nc.gpsimd.tensor_tensor(out=xs[n][:, c0:c1], in0=xc[n][:, c0:c1], in1=sb[:, c0:c1], op=ALU.mult)

        def turn_words(words, part, tag, bufs):
            g0, g1 = part
            np_ = g1 - g0
            xt = psum.tile([P, 512], F32, tag=tag, bufs=bufs, name="xt")
            for gi in range(np_):
                for u in range(2):
                    s = np_ * u + gi
                    lo = 256 * (g0 + gi)
                    nc.tensor.transpose(
                        out=xt[:, 128 * s : 128 * (s + 1)],
                        in_=words[:, lo + u : lo + 256 : 2],
                        identity=ident32[:],
                    )
            return xt

        def turn(n, i):
            banks[(n, i)] = turn_words(xs[n][:].bitcast(F32), pieces(n)[i], "xt", 4)

        def pair_tile(n):
            pr = n // 2
            if pr not in grp:
                if pr in SHARED:
                    grp_pr = held.tile([P, 2 * E], BF16, tag=SHARED[pr], name="grp_s", align_bytes=64)
                else:
                    grp_pr = work.tile([P, 2 * E], BF16, name="grp", align_bytes=64)
                grp[pr] = grp_pr
            return grp[pr], E * (n % 2)

        def so(n, i):
            dst, base = pair_tile(n)
            g0, g1 = pieces(n)[i]
            np_ = g1 - g0
            nc.vector.tensor_tensor(
                out=dst[:, base + 512 * g0 : base + 512 * g1].rearrange(
                    "p (g r u e) -> p g r u e", g=np_, u=2, e=2
                ),
                in0=banks[(n, i)][:, 0 : 256 * np_].bitcast(BF16).rearrange(
                    "p (u g r e) -> p g r u e", u=2, g=np_, e=2
                ),
                in1=sct[:, g0:g1, :].rearrange("p g (o u e) -> p g o u e", o=1, u=2).to_broadcast(
                    [P, np_, 128, 2, 2]
                ),
                op=ALU.mult,
            )

        def words_out(dst, bank):
            nc.scalar.copy(
                out=dst.bitcast(F32).rearrange("p (g r u) -> p g r u", g=2, u=2),
                in_=bank[:].rearrange("p (u g r) -> p g r u", u=2, g=2),
            )

        def evac(n, i):
            dst, base = pair_tile(n)
            g0, g1 = pieces(n)[i]
            words_out(dst[:, base + 512 * g0 : base + 512 * g1], banks[(n, i)])

        def evac_w(n, i):
            if n not in xw:
                xw_n = work.tile([P, E], BF16, name="xw", bufs=2)
                xw[n] = xw_n
            g0, g1 = pieces(n)[i]
            words_out(xw[n][:, 512 * g0 : 512 * g1], banks[(n, i)])

        def gmul_w(n, g0, g1):
            dst, base = pair_tile(n)
            np_ = g1 - g0
            nc.gpsimd.tensor_tensor(
                out=dst[:, base + 512 * g0 : base + 512 * g1].rearrange("p (g r t) -> p g r t", g=np_, t=4),
                in0=xw[n][:, 512 * g0 : 512 * g1].rearrange("p (g r t) -> p g r t", g=np_, t=4),
                in1=sct[:, g0:g1, :].rearrange("p g (o t) -> p g o t", o=1).to_broadcast([P, np_, 128, 4]),
                op=ALU.mult,
            )

        def quant(pr, lo, hi):
            if pr not in codes:
                codes_pr = work.tile([P, E // 2], U32, name="codes", align_bytes=64)
                scales_pr = work.tile([P, E // 2], U8, name="scales", align_bytes=64)
                codes[pr] = codes_pr
                scales[pr] = scales_pr
            nc.vector.quantize_mx(
                out=codes[pr][:, lo // 4 : hi // 4].bitcast(FP8X4),
                scales=scales[pr][:, lo // 4 : hi // 4],
                in_=grp[pr][:, lo:hi],
            )

        def mx(n):
            gi = group_of[n]
            j = n - GROUPS[gi][0]
            if gi not in q_bank:
                if gi < LAST:
                    qp = psum.tile([P, 512], F32, tag="q", bufs=1, name="qp")
                else:
                    qp = psum.tile([P, 512], F32, tag="xt", bufs=4, name="qp")
                q_bank[gi] = qp
            pr = n // 2
            base = 512 * (n % 2)
            for g in range(PASSES):
                gc = slice(128 * g, 128 * (g + 1))
                xc_ = slice(base + 128 * g, base + 128 * (g + 1))
                nc.tensor.matmul_mx(
                    out=q_bank[gi][:, 128 * j : 128 * (j + 1)],
                    lhsT=w_codes[:, gc].bitcast(FP8X4),
                    lhsT_scale=w_scales[:, gc],
                    rhs=codes[pr][:, xc_].bitcast(FP8X4),
                    rhs_scale=scales[pr][:, xc_],
                    start=(g == 0),
                    stop=(g == PASSES - 1),
                )

        def product(gi):
            m = len(GROUPS[gi])
            n0 = GROUPS[gi][0]
            w = 128 * m
            y = work.tile([P, 512], F32, name="y")
            ep[gi]["y"] = y
            if gi not in VECTOR_SUMS:
                nc.vector.scalar_tensor_tensor(
                    out=y[:, 0:w],
                    in0=q_bank[gi][:, 0:w],
                    scalar=bq_col[:, 0:1],
                    in1=g_sb[:, 128 * n0 : 128 * n0 + w],
                    op0=ALU.add,
                    op1=ALU.mult,
                )
            else:
                s1 = small.tile([P, 4], F32, name="s1")
                ep[gi]["s1"] = s1
                for j in range(m):
                    nc.vector.scalar_tensor_tensor(
                        out=y[:, 128 * j : 128 * (j + 1)],
                        in0=q_bank[gi][:, 128 * j : 128 * (j + 1)],
                        scalar=bq_col[:, 0:1],
                        in1=g_sb[:, 128 * (n0 + j) : 128 * (n0 + j + 1)],
                        op0=ALU.add,
                        op1=ALU.mult,
                        accum_out=s1[:, j : j + 1],
                    )

        def turn_back(gi):
            y = ep[gi]["y"]
            if gi < 3:
                yt = psum.tile([P, 512], F32, tag="yt", bufs=2, name="yt")
            else:
                yt = psum.tile([P, 512], F32, tag="xt", bufs=4, name="yt")
            ep[gi]["yt"] = yt
            for j in range(len(GROUPS[gi])):
                nc.tensor.transpose(
                    out=yt[:, 128 * j : 128 * (j + 1)], in_=y[:, 128 * j : 128 * (j + 1)], identity=ident32[:]
                )

        def sums(gi):
            y = ep[gi]["y"]
            s1 = small.tile([P, 4], F32, name="s1")
            ep[gi]["s1"] = s1
            for j in range(len(GROUPS[gi])):
                junk = work.tile([P, 128], F32, name="junk")
                nc.scalar.activation(
                    out=junk[:], in_=y[:, 128 * j : 128 * (j + 1)], func=ACT.Identity, accum_out=s1[:, j : j + 1]
                )

        def stat_bank(gi):
            if gi < LAST:
                st = psum.tile([P, 16], F32, tag="st", bufs=1, name="st")
            else:
                st = psum.tile([P, 16], F32, tag="xt", bufs=4, name="st")
            ep[gi]["st"] = st

        def colsum(gi):
            y = ep[gi]["y"]
            stat_bank(gi)
            for j in range(len(GROUPS[gi])):
                nc.tensor.matmul(
                    out=ep[gi]["st"][:, j : j + 1],
                    lhsT=y[:, 128 * j : 128 * (j + 1)],
                    rhs=one[:, 0:1],
                    start=True,
                    stop=True,
                )

        def cs_copy(gi):
            m = len(GROUPS[gi])
            s1 = small.tile([P, 4], F32, name="s1")
            ep[gi]["s1"] = s1
            nc.scalar.copy(out=s1[:, 0:m], in_=ep[gi]["st"][:, 0:m])

        def stats1(gi):
            m = len(GROUPS[gi])
            if "st" not in ep[gi]:
                stat_bank(gi)
            nc.tensor.matmul(
                out=ep[gi]["st"][:, 4 : 4 + m], lhsT=neg_avg[:], rhs=ep[gi]["s1"][:, 0:m], start=True, stop=True
            )

        def nm_squares(gi):
            m = len(GROUPS[gi])
            y = ep[gi]["y"]
            st = ep[gi]["st"]
            nm = small.tile([P, 4], F32, name="nm")
            ep[gi]["nm"] = nm
            nc.scalar.copy(out=nm[:, 0:m], in_=st[:, 4 : 4 + m])
            s2 = small.tile([P, 4], F32, name="s2")
            ep[gi]["s2"] = s2
            for j in range(m):
                junk = work.tile([P, 128], F32, name="junk")
                nc.scalar.activation(
                    out=junk[:],
                    in_=y[:, 128 * j : 128 * (j + 1)],
                    func=ACT.Square,
                    bias=nm[:, j : j + 1],
                    accum_out=s2[:, j : j + 1],
                )

        def vector_squares(gi):
            y = ep[gi]["y"]
            st = ep[gi]["st"]
            s2 = small.tile([P, 4], F32, name="s2")
            ep[gi]["s2"] = s2
            yc = work.tile([P, 128], F32, name="yc")
            nc.vector.tensor_scalar(out=yc[:], in0=y[:, 0:128], scalar1=st[:, 4:5], scalar2=None, op0=ALU.add)
            junk = work.tile([P, 128], F32, name="junk")
            nc.vector.scalar_tensor_tensor(
                out=junk[:], in0=yc[:], scalar=1.0, in1=yc[:], op0=ALU.mult, op1=ALU.mult, accum_out=s2[:, 0:1]
            )
            ep[gi]["y"] = yc

        def stats2(gi):
            m = len(GROUPS[gi])
            st = ep[gi]["st"]
            nc.tensor.matmul(out=st[:, 8 : 8 + m], lhsT=pos_avg[:], rhs=ep[gi]["s2"][:, 0:m], start=True, stop=True)

        def sdev(gi):
            m = len(GROUPS[gi])
            st = ep[gi]["st"]
            rs = small.tile([P, 4], F32, name="rs")
            ep[gi]["rs"] = rs
            nc.scalar.activation(
                out=rs[:, 0:m], in_=st[:, 8 : 8 + m], func=ACT.Abs_reciprocal_sqrt, bias=eps[:, 0:1]
            )

        def factors(gi):
            m = len(GROUPS[gi])
            if gi < LAST:
                nr = small.tile([P, 4], F32, name="nr")
                ep[gi]["nr"] = nr
                for j in range(m):
                    if not (gi == LAST - 1 and j == m - 1):
                        nc.scalar.activation(
                            out=nr[:, j : j + 1],
                            in_=ep[gi]["nm"][:, j : j + 1],
                            func=ACT.Copy,
                            scale=ep[gi]["rs"][:, j : j + 1],
                        )

        def finish(gi):
            m = len(GROUPS[gi])
            n0 = GROUPS[gi][0]
            o = work.tile([P, 4, 128], F32, name="o")
            for j in range(m):
                yt_j = ep[gi]["yt"][:, 128 * j : 128 * (j + 1)]
                if gi == LAST:
                    nc.vector.tensor_scalar(
                        out=o[:, j, :], in0=yt_j, scalar1=ep[gi]["rs"][:, j : j + 1], scalar2=None, op0=ALU.mult
                    )
                elif gi == LAST - 1 and j == m - 1:
                    nc.vector.tensor_scalar(
                        out=o[:, j, :],
                        in0=yt_j,
                        scalar1=ep[gi]["nm"][:, j : j + 1],
                        scalar2=ep[gi]["rs"][:, j : j + 1],
                        op0=ALU.add,
                        op1=ALU.mult,
                    )
                else:
                    nc.scalar.activation(
                        out=o[:, j, :],
                        in_=yt_j,
                        func=ACT.Identity,
                        scale=ep[gi]["rs"][:, j : j + 1],
                        bias=ep[gi]["nr"][:, j : j + 1],
                    )
            nc.sync.dma_start(out=out[n0 : n0 + m].rearrange("n l q -> l n q"), in_=o[:, 0:m, :])

        def kv_turn(c):
            kt = psum.tile([P, 512], BF16, tag="yt", bufs=2, name="kt")
            kv_state["ps"] = kt
            for j in range(4):
                nc.tensor.transpose(
                    out=kt[:, 128 * j : 128 * (j + 1)], in_=kv_sb[:, 4 * c + j, :], identity=ident16[:]
                )

        def kv_copy(c):
            kv_t = work.tile([P, 512], BF16, name="kv_t")
            kv_state[c] = kv_t
            nc.scalar.copy(out=kv_t[:], in_=kv_state["ps"][:])

        def g_matmul(c):
            gp = psum.tile([P, 512], F32, tag="yt", bufs=2, name="gp")
            kv_state["gp"] = gp
            nc.tensor.matmul(out=gp[:], lhsT=d_t[:], rhs=kv_state[c][:], start=True, stop=True)

        def g_copy(c):
            nc.scalar.copy(out=g_sb[:, 512 * c : 512 * (c + 1)], in_=kv_state["gp"][:])

        def weights_turn(h):
            banks[("w", h)] = turn_words(w_sb[:].bitcast(F32), (2 * h, 2 * h + 2), "yt", 2)

        def weights_out(h):
            words_out(w_grouped[:, HALF * h : HALF * (h + 1)], banks[("w", h)])

        def decay_turn():
            dt_ps = psum.tile([P, 512], BF16, tag="yt", bufs=2, name="dt_ps")
            kv_state["dt"] = dt_ps
            nc.tensor.transpose(out=dt_ps[:, 0:P], in_=d_sb[:], identity=ident16[:])

        def decay_copy():
            nc.scalar.copy(out=d_t[:], in_=kv_state["dt"][:, 0:P])

        vcast_first(0)
        cast(0, 1)
        vcast_piece(0, 2)
        cast(0, 3)
        turn(0, 0)
        turn(0, 1)
        turn(0, 2)
        so(0, 0)
        turn(0, 3)
        cast(1, 0)
        so(0, 1)
        turn(1, 0)
        cast(1, 1)
        gcast(7, 0, E)
        so(0, 2)
        turn(1, 1)
        cast(3, 1)
        so(0, 3)
        turn(3, 1)
        cast(2, 0)
        evac_w(3, 1)
        so(1, 0)
        turn(2, 0)
        cast(2, 1)
        gmul_w(3, 2, 4)
        so(1, 1)
        turn(2, 1)
        cast(3, 0)
        so(2, 0)
        turn(3, 0)
        cast(4, 0)
        so(2, 1)
        weights_turn(0)
        weights_turn(1)
        weights_out(0)
        cast(4, 1)
        so(3, 0)
        weights_out(1)
        cast(5, 0)
        cast(5, 1)
        quant(0, 0, 2 * E)
        turn(4, 0)
        turn(4, 1)
        decay_turn()
        decay_copy()
        kv_turn(0)
        kv_copy(0)
        quant(1, 0, 2 * E)
        turn(5, 0)
        g_matmul(0)
        g_copy(0)
        cast(6, 0)
        cast(6, 1)
        turn(5, 1)
        nc.vector.quantize_mx(out=w_codes[:].bitcast(FP8X4), scales=w_scales[:], in_=w_grouped[:])
        mx(0)
        mx(1)
        mx(2)
        mx(3)

        def members(j):
            if j < 3:
                return 4 * j, 4 * j + 1, 4 * j + 2, 4 * j + 3
            return 12, 13, 15, 14

        def gpsimd_road(c, token):
            if token:
                gmul(c, 0, K_PASS)
                gmul(c, K_PASS, HALF)
            else:
                gmul(c, 0, HALF)

        for j in (1, 2):
            a, b, d, c = members(j)
            a2, b2, d2, c2 = members(j + 1)
            g = j - 1
            so(a, 0)
            gpsimd_road(c, False)
            cast(a2, 0)
            kv_turn(j)
            so(a, 1)
            if j > 1:
                product(g)
            cast(a2, 1)
            turn(d, 0)
            kv_copy(j)
            gmul(c, HALF, E)
            gcast(c2, 0, E)
            turn(d, 1)
            if j > 1:
                colsum(g)
            so(b, 0)
            if j == 1:
                product(g)
            cast(b2, 0)
            turn(c, 0)
            if j == 1:
                colsum(g)
            so(b, 1)
            cast(b2, 1)
            evac(c, 0)
            cs_copy(g)
            turn(c, 1)
            turn_back(g)
            stats1(g)
            g_matmul(j)
            so(d, 0)
            if j == 1:
                cast(d2, 0)
            evac(c, 1)
            nm_squares(g)
            so(d, 1)
            turn(a2, 0)
            turn(a2, 1)
            turn(b2, 0)
            stats2(g)
            g_copy(j)
            quant(a // 2, 0, 2 * E)
            if j == 1:
                cast(d2, 1)
            sdev(g)
            turn(b2, 1)
            quant(d // 2, 0, 2 * E)
            mx(a)
            mx(b)
            factors(g)
            mx(d)
            mx(c)
            finish(g)

        so(12, 0)
        gpsimd_road(14, False)
        cast(15, 0)
        kv_turn(3)
        so(12, 1)
        cast(15, 1)
        product(2)
        gmul(14, HALF, E)
        kv_copy(3)
        turn(15, 0)
        so(13, 0)
        sums(2)
        turn(14, 0)
        g_matmul(3)
        evac(14, 0)
        turn_back(2)
        stats1(2)
        so(13, 1)
        nm_squares(2)
        turn(15, 1)
        turn(14, 1)
        evac(14, 1)
        so(15, 0)
        quant(6, 0, 2 * E)
        stats2(2)
        g_copy(3)
        sdev(2)
        mx(12)
        mx(13)
        quant(7, 0, E)
        factors(2)
        finish(2)
        so(15, 1)
        mx(14)
        quant(7, E, E + HALF)
        quant(7, E + HALF, 2 * E)
        mx(15)
        product(3)
        stats1(3)
        nm_squares(3)
        product(4)
        stats1(4)
        vector_squares(4)
        turn_back(3)
        turn_back(4)
        stats2(3)
        sdev(3)
        stats2(4)
        sdev(4)
        factors(3)
        finish(3)
        factors(4)
        finish(4)
